import numpy as np
import ml_dtypes


def mxq(x, axis, fmt="e4m3"):
    dtype, down = {"e4m3": (ml_dtypes.float8_e4m3fn, 7), "e5m2": (ml_dtypes.float8_e5m2, 14)}[fmt]
    v = np.moveaxis(np.asarray(x, np.float32).astype(ml_dtypes.bfloat16).astype(np.float64), axis, -1)
    blocks = v.reshape(v.shape[:-1] + (-1, 32))
    amax = np.abs(blocks).max(-1, keepdims=True)
    byte = np.maximum(np.where(amax > 0, np.frexp(amax)[1] - 1 + 127, 0) - down, 1)
    scale = np.exp2(byte - 127.0)
    codes = (blocks / scale).astype(np.float32).astype(dtype).astype(np.float64)
    return np.moveaxis((codes * scale).reshape(v.shape), -1, axis)


WIDE = False


def mx_kscale(k):
    if not WIDE:
        return np.ones(k)
    levels = np.array([20, -20, 10, -10, 0])
    a = np.random.permutation(np.resize(levels, k // 512 * 4)).reshape(k // 512, 4)
    idx = np.arange(k)
    return np.exp2(a[idx // 512, idx % 128 // 32])


BF16 = ml_dtypes.bfloat16


def bf(x):
    return np.asarray(x, np.float32).astype(BF16)


def f64(x):
    return np.asarray(x).astype(np.float64)


B, IN_CH, OUT_CH, KH, KW, H, W_IN = 4, 32, 512, 2, 2, 65, 65
HO, WO = H - KH + 1, W_IN - KW + 1
L = HO * WO
KD = KH * KW
F = IN_CH * KD * KD


def setup_inputs():
    s = mx_kscale(OUT_CH)
    x = np.random.standard_normal((B, IN_CH, H, W_IN))
    W = np.random.standard_normal((OUT_CH, F)) / np.sqrt(F) / s[:, None]
    g = (np.random.standard_normal((B, OUT_CH, HO, WO))
         * np.exp2(np.random.randint(-12, 1, (B, 1, HO, WO))) * s[None, :, None, None])
    return {"x": bf(x), "W": bf(W), "grad_out": bf(g)}


def _unfold(x):
    patches = np.stack([x[:, :, i:i + HO, j:j + WO] for i in range(KH) for j in range(KW)], axis=2)
    return patches.reshape(B, IN_CH, KD, L).transpose(0, 3, 1, 2)


def reference(x, W, grad_out):
    g = f64(grad_out).reshape(B, OUT_CH, L)
    dfeat = mxq(g, 1, "e5m2").transpose(0, 2, 1) @ mxq(f64(W), 0, "e4m3")
    d = dfeat.reshape(B, L, IN_CH, KD, KD)
    p = _unfold(f64(x))
    dp = ((d + d.transpose(0, 1, 2, 4, 3)) * p[:, :, :, None, :]).sum(axis=-1)
    dp = dp.transpose(0, 2, 3, 1).reshape(B, IN_CH, KD, HO, WO)
    gx = np.zeros((B, IN_CH, H, W_IN))
    for i in range(KH):
        for j in range(KW):
            gx[:, :, i:i + HO, j:j + WO] += dp[:, :, i * KW + j]
    return gx

@@ -1,0 +1,225 @@
+from contextlib import ExitStack
+
+import concourse.bass as bass
+import concourse.mybir as mybir
+import concourse.tile as tile
+from concourse.masks import make_identity
+
+F32 = mybir.dt.float32
+BF16 = mybir.dt.bfloat16
+U32 = mybir.dt.uint32
+U8 = mybir.dt.uint8
+I32 = mybir.dt.int32
+E4X4 = mybir.dt.float8_e4m3fn_x4
+E5X4 = mybir.dt.float8_e5m2_x4
+ADD = mybir.AluOpType.add
+MULT = mybir.AluOpType.mult
+
+FLOPS = 2 * 4 * 4096 * 512 * 512
+
+P = 128
+NIMG = 4
+CH = 32
+GRID = 64
+XW = 65
+FRAME = 66
+NBLK = 33
+CODE_ROWS = 265
+XR_ROWS = 266
+
+PASSES = (
+    (0, 0, False), (0, 0, True), (0, 1, False), (0, 1, True),
+    (1, 0, False), (1, 0, True),
+    (-1, 1, False), (-1, 1, True),
+)
+DYS = (0, 1, -1)
+
+
+def row_segments(b):
+    segs = []
+    for k in range(8):
+        n, r = divmod(8 * b + k, FRAME)
+        if r == XW:
+            continue
+        if segs and segs[-1][2] == n and segs[-1][0] + segs[-1][1] == k:
+            last = segs[-1]
+            segs[-1] = (last[0], last[1] + 1, last[2], last[3])
+        else:
+            segs.append((k, 1, n, r))
+    return segs
+
+
+def tile_fast2order_de_conv_t_kernel(tc, x, W, grad_out, out):
+    nc = tc.nc
+    with ExitStack() as ctx:
+        keep = ctx.enter_context(tc.tile_pool(name="keep", bufs=1))
+        rawp = ctx.enter_context(tc.tile_pool(name="rawp", bufs=4))
+        grpp = ctx.enter_context(tc.tile_pool(name="grpp", bufs=4))
+        epool = ctx.enter_context(tc.tile_pool(name="epool", bufs=3))
+        opool = ctx.enter_context(tc.tile_pool(name="opool", bufs=2))
+        tps = ctx.enter_context(tc.psum_pool(name="tps", bufs=5))
+        fps = ctx.enter_context(tc.psum_pool(name="fps", bufs=1))
+
+        g_codes = keep.tile([P, CODE_ROWS * GRID], U32, align_bytes=64)
+        g_scales = keep.tile([P, CODE_ROWS * GRID], U8, align_bytes=64)
+        xr = keep.tile([P, XR_ROWS * XW], BF16)
+        w_raw = keep.tile([P, 4, 512], BF16)
+        w_grp = keep.tile([P, 4096], BF16, align_bytes=64)
+        w_codes = keep.tile([P, 1024], U32, align_bytes=64)
+        w_scales = keep.tile([P, 1024], U8, align_bytes=64)
+        ident = keep.tile([P, P], F32)
+        z_a = keep.tile([P, 1024], F32)
+        z_b = keep.tile([P, 1024], F32)
+        ob_a = keep.tile([P, 8, XW], F32)
+        ob_b = keep.tile([P, 8, XW], F32)
+        z_tiles = (z_a, z_b)
+        ob_tiles = (ob_a, ob_b)
+
+        nc.scalar.dma_start(out=w_raw[:], in_=W.rearrange("(p t) f -> p t f", t=4))
+
+        pads = [(0, 1)] + [(FRAME * n + XW, 2) for n in range(NIMG)]
+        for row0, cnt in pads:
+            cols = slice(row0 * GRID, (row0 + cnt) * GRID)
+            nc.vector.memset(g_codes[:, cols].bitcast(I32), 0)
+            nc.vector.memset(g_scales[:, cols].bitcast(I32), 0)
+
+        img = FRAME * XW
+        nc.gpsimd.memset(xr[:, 0:96], 0.0)
+        for n in range(NIMG):
+            lo = XW + img * n + XW * XW - 32
+            hi = XW + img * (n + 1) + 32 if n < NIMG - 1 else XR_ROWS * XW
+            nc.gpsimd.memset(xr[:, lo:hi], 0.0)
+
+        def load_x(n):
+            for q in range(4):
+                off = XW + img * n - (q % 2)
+                nc.scalar.dma_start(
+                    out=xr[CH * q:CH * (q + 1), off:off + XW * XW],
+                    in_=x[n].rearrange("c r s -> c (r s)"),
+                )
+
+        xr_rows = xr[:].rearrange("p (r s) -> p r s", s=XW)
+
+        make_identity(nc, ident[:])
+        for t in z_tiles:
+            nc.gpsimd.memset(t[:], 0.0)
+        for t in ob_tiles:
+            nc.gpsimd.memset(t[:], 0.0)
+
+        w_view = w_raw[:].rearrange("p t (c a b) -> p t c a b", a=4, b=4)
+        for k, (dy, iy, transposed) in enumerate(PASSES):
+            for iz in range(2):
+                i_idx = 2 * iy + iz
+                j0 = 2 * (iy + dy)
+                if transposed:
+                    src = w_view[:, :, :, j0:j0 + 2, i_idx]
+                else:
+                    src = w_view[:, :, :, i_idx, j0:j0 + 2]
+                base = (k * P + iz * 64) * 4
+                nc.vector.tensor_copy(
+                    out=w_grp[:, base:base + 256].rearrange("p (j c t) -> p j c t", j=2, t=4),
+                    in_=src.rearrange("p t c j -> p j c t"),
+                )
+        nc.vector.quantize_mx(out=w_codes[:].bitcast(E4X4), scales=w_scales[:], in_=w_grp[:])
+
+        raw_now = [None]
+
+        def produce_unit(g):
+            n, j = divmod(g, 8)
+            if j % 2 == 0:
+                raw = rawp.tile([P, 4, 1024], BF16, name="raw")
+                nc.sync.dma_start(
+                    out=raw[:],
+                    in_=grad_out[n].rearrange("(p t) y z -> p t (y z)", t=4)[:, :, 512 * j:512 * j + 1024],
+                )
+                raw_now[0] = raw
+            raw = raw_now[0]
+            off = 512 * (j % 2)
+            grouped = grpp.tile([P, 2048], BF16, name="grouped", align_bytes=64)
+            nc.scalar.copy(
+                out=grouped[:].rearrange("p (c i t) -> p c t i", i=4, t=4),
+                in_=raw[:, :, off:off + 512].rearrange("p t (c i) -> p c t i", i=4),
+            )
+            col0 = (FRAME * n + 1 + 8 * j) * GRID
+            nc.vector.quantize_mx(
+                out=g_codes[:, col0:col0 + 512].bitcast(E5X4),
+                scales=g_scales[:, col0:col0 + 512],
+                in_=grouped[:],
+            )
+
+        def block(b):
+            e_tiles = {}
+            for dy in DYS:
+                acc = tps.tile([P, 512], F32, name="acc")
+                mine = [k for k in range(8) if PASSES[k][0] == dy]
+                for pos, k in enumerate(mine):
+                    w0 = (8 * b + 1 - PASSES[k][1]) * GRID
+                    nc.tensor.matmul_mx(
+                        out=acc[:],
+                        lhsT=w_codes[:, k * P:(k + 1) * P].bitcast(E4X4),
+                        lhsT_scale=w_scales[:, k * P:(k + 1) * P],
+                        rhs=g_codes[:, w0:w0 + 512].bitcast(E5X4),
+                        rhs_scale=g_scales[:, w0:w0 + 512],
+                        start=(pos == 0),
+                        stop=(pos == len(mine) - 1),
+                    )
+                e = epool.tile([P, 512], F32, name="e%d" % (dy + 1))
+                r0 = 1 + 8 * b + dy
+                nc.vector.tensor_tensor(
+                    out=e[:].rearrange("p (r u) -> p r u", u=GRID),
+                    in0=acc[:].rearrange("p (r u) -> p r u", u=GRID),
+                    in1=xr_rows[:, r0:r0 + 8, 0:GRID],
+                    op=MULT,
+                )
+                e_tiles[dy] = e
+            q = e_tiles[0]
+            nc.gpsimd.tensor_tensor(out=q[:], in0=q[:], in1=e_tiles[1][:], op=ADD)
+            nc.gpsimd.tensor_tensor(out=q[:], in0=q[:], in1=e_tiles[-1][:], op=ADD)
+            return q
+
+        def first_level(b, q):
+            z = z_tiles[(b // 4) % 2]
+            ps2 = fps.tile([P, 512], F32, name="ps2")
+            for pr in range(4):
+                nc.tensor.transpose(out=ps2[:, pr * P:(pr + 1) * P], in_=q[:, pr * P:(pr + 1) * P], identity=ident[:])
+            ps2_v = ps2[:].rearrange("p (q i j c) -> p q i j c", q=4, i=2, j=2)
+            z_v = z[:].rearrange("p (q i k c) -> p q i k c", q=4, i=2, k=4)[:, :, :, b % 4, :]
+            nc.scalar.copy(out=z_v, in_=ps2_v[:, :, :, 0, :])
+            nc.vector.tensor_tensor(out=z_v, in0=ps2_v[:, :, :, 1, :], in1=z_v, op=ADD)
+
+        def second_level(sb, nblk):
+            z = z_tiles[sb % 2]
+            ob = ob_tiles[sb % 2]
+            ps3a = fps.tile([P, 512], F32, name="ps3a")
+            ps3b = fps.tile([P, 512], F32, name="ps3b")
+            for pr in range(4):
+                nc.tensor.transpose(out=ps3a[:, pr * P:(pr + 1) * P], in_=z[:, pr * 256:pr * 256 + P], identity=ident[:])
+            for pr in range(4):
+                nc.tensor.transpose(out=ps3b[:, pr * P:(pr + 1) * P], in_=z[:, pr * 256 + P:pr * 256 + 2 * P], identity=ident[:])
+            nc.scalar.copy(out=ob[:, :, 1:XW], in_=ps3b[:].rearrange("p (r u) -> p r u", u=GRID))
+            o = opool.tile([P, 8, XW], F32, name="o")
+            nc.vector.tensor_tensor(
+                out=o[:, :, 0:GRID],
+                in0=ps3a[:].rearrange("p (r u) -> p r u", u=GRID),
+                in1=ob[:, :, 0:GRID],
+                op=ADD,
+            )
+            nc.vector.tensor_copy(out=o[:, :, GRID:XW], in_=ob[:, :, GRID:XW])
+            for k in range(nblk):
+                for k0, cnt, n, r0 in row_segments(4 * sb + k):
+                    nc.sync.dma_start(
+                        out=out[n, :, r0:r0 + cnt, :],
+                        in_=o[CH * k:CH * (k + 1), k0:k0 + cnt, :],
+                    )
+
+        for b in range(NBLK):
+            if b < 32:
+                produce_unit(b)
+            if b == 0:
+                load_x(0)
+            if b in (2, 4, 6):
+                load_x(b // 2)
+            q = block(b)
+            first_level(b, q)
+            if b % 4 == 3 or b == NBLK - 1:
+                second_level(b // 4, b % 4 + 1)

@@ -75,36 +75,57 @@ def tile_fast2order_de_conv_t_kernel(tc, x, W, grad_out, out):
         z_tiles = (z_a, z_b)
         ob_tiles = (ob_a, ob_b)
 
-        nc.scalar.dma_start(out=w_raw[:], in_=W.rearrange("(p t) f -> p t f", t=4))
-
-        pads = [(0, 1)] + [(FRAME * n + XW, 2) for n in range(NIMG)]
-        for row0, cnt in pads:
-            cols = slice(row0 * GRID, (row0 + cnt) * GRID)
-            nc.vector.memset(g_codes[:, cols].bitcast(I32), 0)
-            nc.vector.memset(g_scales[:, cols].bitcast(I32), 0)
+        make_identity(nc, ident[:])
+        ctx.enter_context(tc.manual_schedule())
 
         img = FRAME * XW
+        xr_rows = xr[:].rearrange("p (r s) -> p r s", s=XW)
+        raws = {}
+        groups = {}
+        qs = {}
+        ps2s = {}
+        ps3s = {}
+
+        def load_chunk(c, pieces):
+            n, h = divmod(c, 4)
+            raw = rawp.tile([P, 4, 1024], BF16, name="raw")
+            src = grad_out[n].rearrange("(p t) y z -> p t (y z)", t=4)
+            w = 1024 // pieces
+            for k in range(pieces):
+                nc.sync.dma_start(
+                    out=raw[:, :, k * w:(k + 1) * w],
+                    in_=src[:, :, 1024 * h + k * w:1024 * h + (k + 1) * w],
+                )
+            raws[c] = raw
+
+        def load_x(n):
+            for q in range(4):
+                off = XW + img * n - (q % 2)
+                nc.sync.dma_start(
+                    out=xr[CH * q:CH * (q + 1), off:off + XW * XW],
+                    in_=x[n].rearrange("c r s -> c (r s)"),
+                )
+
+        nc.scalar.dma_start(out=w_raw[:], in_=W.rearrange("(p t) f -> p t f", t=4))
         nc.gpsimd.memset(xr[:, 0:96], 0.0)
         for n in range(NIMG):
             lo = XW + img * n + XW * XW - 32
             hi = XW + img * (n + 1) + 32 if n < NIMG - 1 else XR_ROWS * XW
             nc.gpsimd.memset(xr[:, lo:hi], 0.0)
-
-        def load_x(n):
-            for q in range(4):
-                off = XW + img * n - (q % 2)
-                nc.scalar.dma_start(
-                    out=xr[CH * q:CH * (q + 1), off:off + XW * XW],
-                    in_=x[n].rearrange("c r s -> c (r s)"),
-                )
-
-        xr_rows = xr[:].rearrange("p (r s) -> p r s", s=XW)
-
-        make_identity(nc, ident[:])
+        load_chunk(0, 2)
+        load_x(0)
+        load_chunk(1, 1)
+        load_chunk(2, 1)
+        load_chunk(3, 1)
         for t in z_tiles:
             nc.gpsimd.memset(t[:], 0.0)
         for t in ob_tiles:
             nc.gpsimd.memset(t[:], 0.0)
+        pads = [(0, 1)] + [(FRAME * n + XW, 2) for n in range(NIMG)]
+        for row0, cnt in pads:
+            cols = slice(row0 * GRID, (row0 + cnt) * GRID)
+            nc.vector.memset(g_codes[:, cols].bitcast(I32), 0)
+            nc.vector.memset(g_scales[:, cols].bitcast(I32), 0)
 
         w_view = w_raw[:].rearrange("p t (c a b) -> p t c a b", a=4, b=4)
         for k, (dy, iy, transposed) in enumerate(PASSES):
@@ -122,29 +143,25 @@ def tile_fast2order_de_conv_t_kernel(tc, x, W, grad_out, out):
                 )
         nc.vector.quantize_mx(out=w_codes[:].bitcast(E4X4), scales=w_scales[:], in_=w_grp[:])
 
-        raw_now = [None]
-
-        def produce_unit(g):
-            n, j = divmod(g, 8)
-            if j % 2 == 0:
-                raw = rawp.tile([P, 4, 1024], BF16, name="raw")
-                nc.sync.dma_start(
-                    out=raw[:],
-                    in_=grad_out[n].rearrange("(p t) y z -> p t (y z)", t=4)[:, :, 512 * j:512 * j + 1024],
-                )
-                raw_now[0] = raw
-            raw = raw_now[0]
-            off = 512 * (j % 2)
+        def regroup(u):
+            raw = raws[u // 2]
+            off = 512 * (u % 2)
             grouped = grpp.tile([P, 2048], BF16, name="grouped", align_bytes=64)
             nc.scalar.copy(
                 out=grouped[:].rearrange("p (c i t) -> p c t i", i=4, t=4),
                 in_=raw[:, :, off:off + 512].rearrange("p t (c i) -> p c t i", i=4),
             )
+            groups[u] = grouped
+            if u % 2 == 1 and u // 2 + 4 < 16:
+                load_chunk(u // 2 + 4, 1)
+
+        def quantise(u):
+            n, j = divmod(u, 8)
             col0 = (FRAME * n + 1 + 8 * j) * GRID
             nc.vector.quantize_mx(
                 out=g_codes[:, col0:col0 + 512].bitcast(E5X4),
                 scales=g_scales[:, col0:col0 + 512],
-                in_=grouped[:],
+                in_=groups[u][:],
             )
 
         def block(b):
@@ -172,54 +189,82 @@ def tile_fast2order_de_conv_t_kernel(tc, x, W, grad_out, out):
                     op=MULT,
                 )
                 e_tiles[dy] = e
-            q = e_tiles[0]
-            nc.gpsimd.tensor_tensor(out=q[:], in0=q[:], in1=e_tiles[1][:], op=ADD)
-            nc.gpsimd.tensor_tensor(out=q[:], in0=q[:], in1=e_tiles[-1][:], op=ADD)
-            return q
+                if dy == 1:
+                    nc.gpsimd.tensor_tensor(out=e_tiles[0][:], in0=e_tiles[0][:], in1=e[:], op=ADD)
+                if dy == -1:
+                    nc.gpsimd.tensor_tensor(out=e_tiles[0][:], in0=e_tiles[0][:], in1=e[:], op=ADD)
+            qs[b] = e_tiles[0]
 
-        def first_level(b, q):
-            z = z_tiles[(b // 4) % 2]
+        def first_t(b):
+            q = qs[b]
             ps2 = fps.tile([P, 512], F32, name="ps2")
             for pr in range(4):
                 nc.tensor.transpose(out=ps2[:, pr * P:(pr + 1) * P], in_=q[:, pr * P:(pr + 1) * P], identity=ident[:])
-            ps2_v = ps2[:].rearrange("p (q i j c) -> p q i j c", q=4, i=2, j=2)
-            z_v = z[:].rearrange("p (q i k c) -> p q i k c", q=4, i=2, k=4)[:, :, :, b % 4, :]
-            nc.scalar.copy(out=z_v, in_=ps2_v[:, :, :, 0, :])
-            nc.vector.tensor_tensor(out=z_v, in0=ps2_v[:, :, :, 1, :], in1=z_v, op=ADD)
+            ps2s[b] = ps2
 
-        def second_level(sb, nblk):
+        def z_view(b):
+            z = z_tiles[(b // 4) % 2]
+            return z[:].rearrange("p (q i k c) -> p q i k c", q=4, i=2, k=4)[:, :, :, b % 4, :]
+
+        def ps2_view(b, jz):
+            return ps2s[b][:].rearrange("p (q i j c) -> p q i j c", q=4, i=2, j=2)[:, :, :, jz, :]
+
+        def evac2_copy(b):
+            nc.scalar.copy(out=z_view(b), in_=ps2_view(b, 0))
+
+        def z_add(b):
+            nc.vector.tensor_tensor(out=z_view(b), in0=ps2_view(b, 1), in1=z_view(b), op=ADD)
+
+        def second_t(sb):
             z = z_tiles[sb % 2]
-            ob = ob_tiles[sb % 2]
             ps3a = fps.tile([P, 512], F32, name="ps3a")
             ps3b = fps.tile([P, 512], F32, name="ps3b")
             for pr in range(4):
-                nc.tensor.transpose(out=ps3a[:, pr * P:(pr + 1) * P], in_=z[:, pr * 256:pr * 256 + P], identity=ident[:])
-            for pr in range(4):
                 nc.tensor.transpose(out=ps3b[:, pr * P:(pr + 1) * P], in_=z[:, pr * 256 + P:pr * 256 + 2 * P], identity=ident[:])
-            nc.scalar.copy(out=ob[:, :, 1:XW], in_=ps3b[:].rearrange("p (r u) -> p r u", u=GRID))
+            for pr in range(4):
+                nc.tensor.transpose(out=ps3a[:, pr * P:(pr + 1) * P], in_=z[:, pr * 256:pr * 256 + P], identity=ident[:])
+            ps3s[sb] = (ps3a, ps3b)
+
+        def ps3_copy(sb):
+            nc.scalar.copy(out=ob_tiles[sb % 2][:, :, 1:XW], in_=ps3s[sb][1][:].rearrange("p (r u) -> p r u", u=GRID))
+
+        def final(sb):
+            ob = ob_tiles[sb % 2]
             o = opool.tile([P, 8, XW], F32, name="o")
             nc.vector.tensor_tensor(
                 out=o[:, :, 0:GRID],
-                in0=ps3a[:].rearrange("p (r u) -> p r u", u=GRID),
+                in0=ps3s[sb][0][:].rearrange("p (r u) -> p r u", u=GRID),
                 in1=ob[:, :, 0:GRID],
                 op=ADD,
             )
             nc.vector.tensor_copy(out=o[:, :, GRID:XW], in_=ob[:, :, GRID:XW])
-            for k in range(nblk):
+            for k in range(min(4, NBLK - 4 * sb)):
                 for k0, cnt, n, r0 in row_segments(4 * sb + k):
                     nc.sync.dma_start(
                         out=out[n, :, r0:r0 + cnt, :],
                         in_=o[CH * k:CH * (k + 1), k0:k0 + cnt, :],
                     )
 
-        for b in range(NBLK):
-            if b < 32:
-                produce_unit(b)
-            if b == 0:
-                load_x(0)
-            if b in (2, 4, 6):
-                load_x(b // 2)
-            q = block(b)
-            first_level(b, q)
-            if b % 4 == 3 or b == NBLK - 1:
-                second_level(b // 4, b % 4 + 1)
+        last_of = {min(4 * sb + 3, NBLK - 1): sb for sb in range((NBLK + 3) // 4)}
+
+        for s in range(-2, NBLK + 5):
+            if 0 <= s - 3 < NBLK:
+                evac2_copy(s - 3)
+            if (s - 4) in last_of:
+                ps3_copy(last_of[s - 4])
+            if 0 <= s + 2 < 32:
+                regroup(s + 2)
+            if s in (2, 10, 18):
+                load_x((s + 6) // 8)
+            if 0 <= s + 1 < 32:
+                quantise(s + 1)
+            if 0 <= s - 3 < NBLK:
+                z_add(s - 3)
+            if (s - 4) in last_of:
+                final(last_of[s - 4])
+            if 0 <= s < NBLK:
+                block(s)
+            if 0 <= s - 2 < NBLK:
+                first_t(s - 2)
+            if (s - 3) in last_of:
+                second_t(last_of[s - 3])

@@ -28,11 +28,9 @@ CODE_ROWS = 265
 XR_ROWS = 266
 
 PASSES = (
-    (0, 0, False), (0, 0, True), (0, 1, False), (0, 1, True),
     (1, 0, False), (1, 0, True),
-    (-1, 1, False), (-1, 1, True),
+    (0, 0, False), (0, 0, True), (0, 1, False), (0, 1, True),
 )
-DYS = (0, 1, -1)
 
 
 def row_segments(b):
@@ -53,21 +51,21 @@ def tile_fast2order_de_conv_t_kernel(tc, x, W, grad_out, out):
     nc = tc.nc
     with ExitStack() as ctx:
         keep = ctx.enter_context(tc.tile_pool(name="keep", bufs=1))
-        rawp = ctx.enter_context(tc.tile_pool(name="rawp", bufs=4))
-        grpp = ctx.enter_context(tc.tile_pool(name="grpp", bufs=4))
-        epool = ctx.enter_context(tc.tile_pool(name="epool", bufs=3))
-        opool = ctx.enter_context(tc.tile_pool(name="opool", bufs=2))
-        tps = ctx.enter_context(tc.psum_pool(name="tps", bufs=5))
-        fps = ctx.enter_context(tc.psum_pool(name="fps", bufs=1))
+        rawp = ctx.enter_context(tc.tile_pool(name="rawp", bufs=3))
+        grpp = ctx.enter_context(tc.tile_pool(name="grpp", bufs=3))
+        tps = ctx.enter_context(tc.psum_pool(name="tps", bufs=4))
+        fps2 = ctx.enter_context(tc.psum_pool(name="fps2", bufs=2))
+        fps3 = ctx.enter_context(tc.psum_pool(name="fps3", bufs=1))
 
         g_codes = keep.tile([P, CODE_ROWS * GRID], U32, align_bytes=64)
         g_scales = keep.tile([P, CODE_ROWS * GRID], U8, align_bytes=64)
-        xr = keep.tile([P, XR_ROWS * XW], BF16)
-        w_raw = keep.tile([P, 4, 512], BF16)
-        w_grp = keep.tile([P, 4096], BF16, align_bytes=64)
-        w_codes = keep.tile([P, 1024], U32, align_bytes=64)
-        w_scales = keep.tile([P, 1024], U8, align_bytes=64)
+        xr_b = keep.tile([P, XR_ROWS * XW], BF16)
+        xr_a = keep.tile([P, XR_ROWS * XW], BF16)
+        w_codes = keep.tile([P, 768], U32, align_bytes=64)
+        w_scales = keep.tile([P, 768], U8, align_bytes=64)
         ident = keep.tile([P, P], F32)
+        swap = keep.tile([P, P], F32)
+        fring = keep.tile([P, 33 * GRID], F32)
         z_a = keep.tile([P, 1024], F32)
         z_b = keep.tile([P, 1024], F32)
         ob_a = keep.tile([P, 8, XW], F32)
@@ -79,10 +77,11 @@ def tile_fast2order_de_conv_t_kernel(tc, x, W, grad_out, out):
         ctx.enter_context(tc.manual_schedule())
 
         img = FRAME * XW
-        xr_rows = xr[:].rearrange("p (r s) -> p r s", s=XW)
+        xb_rows = xr_b[:].rearrange("p (r s) -> p r s", s=XW)
+        xa_rows = xr_a[:].rearrange("p (r s) -> p r s", s=XW)
         raws = {}
         groups = {}
-        qs = {}
+        es = {}
         ps2s = {}
         ps3s = {}
 
@@ -98,50 +97,65 @@ def tile_fast2order_de_conv_t_kernel(tc, x, W, grad_out, out):
                 )
             raws[c] = raw
 
-        def load_x(n):
+        def load_x(eng, which, n, row0, row1):
+            src = x[n].rearrange("c r s -> c (r s)")[:, row0 * XW:row1 * XW]
             for q in range(4):
-                off = XW + img * n - (q % 2)
-                nc.sync.dma_start(
-                    out=xr[CH * q:CH * (q + 1), off:off + XW * XW],
-                    in_=x[n].rearrange("c r s -> c (r s)"),
-                )
+                for xt, shift in ((xr_b, q % 2), (xr_a, q // 2)):
+                    if xt in which:
+                        off = XW + img * n + row0 * XW - shift
+                        eng.dma_start(out=xt[CH * q:CH * (q + 1), off:off + (row1 - row0) * XW], in_=src)
 
-        nc.scalar.dma_start(out=w_raw[:], in_=W.rearrange("(p t) f -> p t f", t=4))
-        nc.gpsimd.memset(xr[:, 0:96], 0.0)
-        for n in range(NIMG):
-            lo = XW + img * n + XW * XW - 32
-            hi = XW + img * (n + 1) + 32 if n < NIMG - 1 else XR_ROWS * XW
-            nc.gpsimd.memset(xr[:, lo:hi], 0.0)
-        load_chunk(0, 2)
-        load_x(0)
-        load_chunk(1, 1)
-        load_chunk(2, 1)
-        load_chunk(3, 1)
-        for t in z_tiles:
-            nc.gpsimd.memset(t[:], 0.0)
-        for t in ob_tiles:
-            nc.gpsimd.memset(t[:], 0.0)
-        pads = [(0, 1)] + [(FRAME * n + XW, 2) for n in range(NIMG)]
-        for row0, cnt in pads:
-            cols = slice(row0 * GRID, (row0 + cnt) * GRID)
-            nc.vector.memset(g_codes[:, cols].bitcast(I32), 0)
-            nc.vector.memset(g_scales[:, cols].bitcast(I32), 0)
+        wstage = tc.tile_pool(name="wstage", bufs=1)
+        with wstage as wpool:
+            w_raw = wpool.tile([P, 4, 512], BF16)
+            w_grp = wpool.tile([P, 3072], BF16, align_bytes=64)
+            nc.scalar.dma_start(out=w_raw[:], in_=W.rearrange("(p t) f -> p t f", t=4))
+            both = (xr_b, xr_a)
+            for xt in both:
+                nc.gpsimd.memset(xt[:, 0:96], 0.0)
+            load_chunk(0, 2)
+            load_x(nc.gpsimd, (xr_a,), 0, 0, 17)
+            load_x(nc.sync, (xr_b,), 0, 0, 17)
+            for xt in both:
+                for n in range(NIMG):
+                    lo = XW + img * n + XW * XW - 32
+                    hi = XW + img * (n + 1) + 32 if n < NIMG - 1 else XR_ROWS * XW
+                    nc.gpsimd.memset(xt[:, lo:hi], 0.0)
+            load_chunk(1, 1)
+            load_chunk(2, 1)
+            load_x(nc.sync, both, 0, 16, XW)
+            nc.gpsimd.memset(fring[:, 0:GRID], 0.0)
+            for t in z_tiles:
+                nc.gpsimd.memset(t[:], 0.0)
+            for t in ob_tiles:
+                nc.gpsimd.memset(t[:], 0.0)
+            pads = [(0, 1)] + [(FRAME * n + XW, 2) for n in range(NIMG)]
+            for row0, cnt in pads:
+                cols = slice(row0 * GRID, (row0 + cnt) * GRID)
+                nc.vector.memset(g_codes[:, cols].bitcast(I32), 0)
+                nc.vector.memset(g_scales[:, cols].bitcast(I32), 0)
+            nc.vector.tensor_copy(out=swap[:, 0:32], in_=ident[:, 0:32])
+            nc.vector.tensor_copy(out=swap[:, 32:64], in_=ident[:, 64:96])
+            nc.vector.tensor_copy(out=swap[:, 64:96], in_=ident[:, 32:64])
+            nc.vector.tensor_copy(out=swap[:, 96:128], in_=ident[:, 96:128])
 
-        w_view = w_raw[:].rearrange("p t (c a b) -> p t c a b", a=4, b=4)
-        for k, (dy, iy, transposed) in enumerate(PASSES):
-            for iz in range(2):
-                i_idx = 2 * iy + iz
+            w_view = w_raw[:].rearrange("p t (c a b) -> p t c a b", a=4, b=4)
+            for k, (dy, iy, transposed) in enumerate(PASSES):
+                i0 = 2 * iy
                 j0 = 2 * (iy + dy)
                 if transposed:
-                    src = w_view[:, :, :, j0:j0 + 2, i_idx]
+                    src = w_view[:, :, :, j0:j0 + 2, i0:i0 + 2].rearrange("p t c j i -> p i j c t")
                 else:
-                    src = w_view[:, :, :, i_idx, j0:j0 + 2]
-                base = (k * P + iz * 64) * 4
+                    src = w_view[:, :, :, i0:i0 + 2, j0:j0 + 2].rearrange("p t c i j -> p i j c t")
                 nc.vector.tensor_copy(
-                    out=w_grp[:, base:base + 256].rearrange("p (j c t) -> p j c t", j=2, t=4),
-                    in_=src.rearrange("p t c j -> p j c t"),
+                    out=w_grp[:, k * 512:(k + 1) * 512].rearrange("p (i j c t) -> p i j c t", i=2, j=2, t=4),
+                    in_=src,
                 )
-        nc.vector.quantize_mx(out=w_codes[:].bitcast(E4X4), scales=w_scales[:], in_=w_grp[:])
+            nc.vector.quantize_mx(out=w_codes[:, 0:256].bitcast(E4X4), scales=w_scales[:, 0:256], in_=w_grp[:, 0:1024])
+            nc.vector.quantize_mx(out=w_codes[:, 256:768].bitcast(E4X4), scales=w_scales[:, 256:768], in_=w_grp[:, 1024:3072])
+
+        epool = ctx.enter_context(tc.tile_pool(name="epool", bufs=3))
+        opool = ctx.enter_context(tc.tile_pool(name="opool", bufs=2))
 
         def regroup(u):
             raw = raws[u // 2]
@@ -152,8 +166,8 @@ def tile_fast2order_de_conv_t_kernel(tc, x, W, grad_out, out):
                 in_=raw[:, :, off:off + 512].rearrange("p t (c i) -> p c t i", i=4),
             )
             groups[u] = grouped
-            if u % 2 == 1 and u // 2 + 4 < 16:
-                load_chunk(u // 2 + 4, 1)
+            if u % 2 == 1 and u // 2 + 3 < 16:
+                load_chunk(u // 2 + 3, 1)
 
         def quantise(u):
             n, j = divmod(u, 8)
@@ -164,42 +178,47 @@ def tile_fast2order_de_conv_t_kernel(tc, x, W, grad_out, out):
                 in_=groups[u][:],
             )
 
-        def block(b):
-            e_tiles = {}
-            for dy in DYS:
-                acc = tps.tile([P, 512], F32, name="acc")
-                mine = [k for k in range(8) if PASSES[k][0] == dy]
-                for pos, k in enumerate(mine):
-                    w0 = (8 * b + 1 - PASSES[k][1]) * GRID
-                    nc.tensor.matmul_mx(
-                        out=acc[:],
-                        lhsT=w_codes[:, k * P:(k + 1) * P].bitcast(E4X4),
-                        lhsT_scale=w_scales[:, k * P:(k + 1) * P],
-                        rhs=g_codes[:, w0:w0 + 512].bitcast(E5X4),
-                        rhs_scale=g_scales[:, w0:w0 + 512],
-                        start=(pos == 0),
-                        stop=(pos == len(mine) - 1),
-                    )
-                e = epool.tile([P, 512], F32, name="e%d" % (dy + 1))
-                r0 = 1 + 8 * b + dy
-                nc.vector.tensor_tensor(
-                    out=e[:].rearrange("p (r u) -> p r u", u=GRID),
-                    in0=acc[:].rearrange("p (r u) -> p r u", u=GRID),
-                    in1=xr_rows[:, r0:r0 + 8, 0:GRID],
-                    op=MULT,
+        def passes(acc, b, ks):
+            for pos, k in enumerate(ks):
+                w0 = (8 * b + 1 - PASSES[k][1]) * GRID
+                nc.tensor.matmul_mx(
+                    out=acc[:],
+                    lhsT=w_codes[:, k * P:(k + 1) * P].bitcast(E4X4),
+                    lhsT_scale=w_scales[:, k * P:(k + 1) * P],
+                    rhs=g_codes[:, w0:w0 + 512].bitcast(E5X4),
+                    rhs_scale=g_scales[:, w0:w0 + 512],
+                    start=(pos == 0),
+                    stop=(pos == len(ks) - 1),
                 )
-                e_tiles[dy] = e
-                if dy == 1:
-                    nc.gpsimd.tensor_tensor(out=e_tiles[0][:], in0=e_tiles[0][:], in1=e[:], op=ADD)
-                if dy == -1:
-                    nc.gpsimd.tensor_tensor(out=e_tiles[0][:], in0=e_tiles[0][:], in1=e[:], op=ADD)
-            qs[b] = e_tiles[0]
+
+        def rows_of(ap):
+            return ap.rearrange("p (r u) -> p r u", u=GRID)
+
+        def block(b):
+            r0 = 1 + 8 * b
+            alpha = tps.tile([P, 512], F32, name="acc")
+            passes(alpha, b, (0, 1))
+            e1 = epool.tile([P, 512], F32, name="e1")
+            nc.vector.tensor_tensor(out=rows_of(e1[:]), in0=rows_of(alpha[:]), in1=xb_rows[:, r0 + 1:r0 + 9, 0:GRID], op=MULT)
+            f0 = (1 + 8 * (b % 4)) * GRID
+            nc.vector.tensor_tensor(out=rows_of(fring[:, f0:f0 + 512]), in0=rows_of(alpha[:]), in1=xa_rows[:, r0:r0 + 8, 0:GRID], op=MULT)
+            if b % 4 == 3:
+                nc.vector.tensor_tensor(out=fring[:, 0:GRID], in0=alpha[:, 448:512], in1=xr_a[:, (r0 + 7) * XW:(r0 + 7) * XW + GRID], op=MULT)
+            beta = tps.tile([P, 512], F32, name="acc")
+            passes(beta, b, (2, 3, 4, 5))
+            e0 = epool.tile([P, 512], F32, name="e0")
+            nc.vector.tensor_tensor(out=rows_of(e0[:]), in0=rows_of(beta[:]), in1=xb_rows[:, r0:r0 + 8, 0:GRID], op=MULT)
+            es[b] = (e0, e1)
 
         def first_t(b):
-            q = qs[b]
-            ps2 = fps.tile([P, 512], F32, name="ps2")
+            e0, e1 = es[b]
+            ps2 = fps2.tile([P, 512], F32, name="ps2")
             for pr in range(4):
-                nc.tensor.transpose(out=ps2[:, pr * P:(pr + 1) * P], in_=q[:, pr * P:(pr + 1) * P], identity=ident[:])
+                cols = slice(pr * P, (pr + 1) * P)
+                f0 = (8 * (b % 4) + 2 * pr) * GRID
+                nc.tensor.matmul(out=ps2[:, cols], lhsT=e1[:, cols], rhs=ident[:], is_transpose=True, start=True, stop=False)
+                nc.tensor.matmul(out=ps2[:, cols], lhsT=fring[:, f0:f0 + P], rhs=swap[:], is_transpose=True, start=False, stop=False)
+                nc.tensor.matmul(out=ps2[:, cols], lhsT=e0[:, cols], rhs=ident[:], is_transpose=True, start=False, stop=True)
             ps2s[b] = ps2
 
         def z_view(b):
@@ -217,8 +236,8 @@ def tile_fast2order_de_conv_t_kernel(tc, x, W, grad_out, out):
 
         def second_t(sb):
             z = z_tiles[sb % 2]
-            ps3a = fps.tile([P, 512], F32, name="ps3a")
-            ps3b = fps.tile([P, 512], F32, name="ps3b")
+            ps3a = fps3.tile([P, 512], F32, name="ps3a")
+            ps3b = fps3.tile([P, 512], F32, name="ps3b")
             for pr in range(4):
                 nc.tensor.transpose(out=ps3b[:, pr * P:(pr + 1) * P], in_=z[:, pr * 256 + P:pr * 256 + 2 * P], identity=ident[:])
             for pr in range(4):
@@ -226,17 +245,12 @@ def tile_fast2order_de_conv_t_kernel(tc, x, W, grad_out, out):
             ps3s[sb] = (ps3a, ps3b)
 
         def ps3_copy(sb):
-            nc.scalar.copy(out=ob_tiles[sb % 2][:, :, 1:XW], in_=ps3s[sb][1][:].rearrange("p (r u) -> p r u", u=GRID))
+            nc.scalar.copy(out=ob_tiles[sb % 2][:, :, 1:XW], in_=rows_of(ps3s[sb][1][:]))
 
         def final(sb):
             ob = ob_tiles[sb % 2]
             o = opool.tile([P, 8, XW], F32, name="o")
-            nc.vector.tensor_tensor(
-                out=o[:, :, 0:GRID],
-                in0=ps3s[sb][0][:].rearrange("p (r u) -> p r u", u=GRID),
-                in1=ob[:, :, 0:GRID],
-                op=ADD,
-            )
+            nc.vector.tensor_tensor(out=o[:, :, 0:GRID], in0=rows_of(ps3s[sb][0][:]), in1=ob[:, :, 0:GRID], op=ADD)
             nc.vector.tensor_copy(out=o[:, :, GRID:XW], in_=ob[:, :, GRID:XW])
             for k in range(min(4, NBLK - 4 * sb)):
                 for k0, cnt, n, r0 in row_segments(4 * sb + k):
@@ -247,24 +261,24 @@ def tile_fast2order_de_conv_t_kernel(tc, x, W, grad_out, out):
 
         last_of = {min(4 * sb + 3, NBLK - 1): sb for sb in range((NBLK + 3) // 4)}
 
-        for s in range(-2, NBLK + 5):
-            if 0 <= s - 3 < NBLK:
-                evac2_copy(s - 3)
-            if (s - 4) in last_of:
-                ps3_copy(last_of[s - 4])
+        for s in range(-2, NBLK + 4):
+            if 0 <= s - 2 < NBLK:
+                evac2_copy(s - 2)
+            if (s - 3) in last_of:
+                ps3_copy(last_of[s - 3])
             if 0 <= s + 2 < 32:
                 regroup(s + 2)
             if s in (2, 10, 18):
-                load_x((s + 6) // 8)
+                load_x(nc.sync, both, (s + 6) // 8, 0, XW)
             if 0 <= s + 1 < 32:
                 quantise(s + 1)
-            if 0 <= s - 3 < NBLK:
-                z_add(s - 3)
-            if (s - 4) in last_of:
-                final(last_of[s - 4])
+            if 0 <= s - 2 < NBLK:
+                z_add(s - 2)
+            if (s - 3) in last_of:
+                final(last_of[s - 3])
             if 0 <= s < NBLK:
                 block(s)
-            if 0 <= s - 2 < NBLK:
-                first_t(s - 2)
-            if (s - 3) in last_of:
-                second_t(last_of[s - 3])
+            if 0 <= s - 1 < NBLK:
+                first_t(s - 1)
+            if (s - 2) in last_of:
+                second_t(last_of[s - 2])

@@ -208,16 +208,16 @@ def tile_fast2order_de_conv_t_kernel(tc, x, W, grad_out, out):
             passes(beta, b, (2, 3, 4, 5))
             e0 = epool.tile([P, 512], F32, name="e0")
             nc.vector.tensor_tensor(out=rows_of(e0[:]), in0=rows_of(beta[:]), in1=xb_rows[:, r0:r0 + 8, 0:GRID], op=MULT)
-            es[b] = (e0, e1)
+            nc.gpsimd.tensor_tensor(out=e0[:], in0=e0[:], in1=e1[:], op=ADD)
+            es[b] = e0
 
         def first_t(b):
-            e0, e1 = es[b]
+            e0 = es[b]
             ps2 = fps2.tile([P, 512], F32, name="ps2")
             for pr in range(4):
                 cols = slice(pr * P, (pr + 1) * P)
                 f0 = (8 * (b % 4) + 2 * pr) * GRID
-                nc.tensor.matmul(out=ps2[:, cols], lhsT=e1[:, cols], rhs=ident[:], is_transpose=True, start=True, stop=False)
-                nc.tensor.matmul(out=ps2[:, cols], lhsT=fring[:, f0:f0 + P], rhs=swap[:], is_transpose=True, start=False, stop=False)
+                nc.tensor.matmul(out=ps2[:, cols], lhsT=fring[:, f0:f0 + P], rhs=swap[:], is_transpose=True, start=True, stop=False)
                 nc.tensor.matmul(out=ps2[:, cols], lhsT=e0[:, cols], rhs=ident[:], is_transpose=True, start=False, stop=True)
             ps2s[b] = ps2
 

@@ -26,6 +26,7 @@ FRAME = 66
 NBLK = 33
 CODE_ROWS = 265
 XR_ROWS = 266
+S_COLS = 384
 
 PASSES = (
     (1, 0, False), (1, 0, True),
@@ -66,12 +67,15 @@ def tile_fast2order_de_conv_t_kernel(tc, x, W, grad_out, out):
         ident = keep.tile([P, P], F32)
         swap = keep.tile([P, P], F32)
         fring = keep.tile([P, 33 * GRID], F32)
-        z_a = keep.tile([P, 1024], F32)
-        z_b = keep.tile([P, 1024], F32)
+        z_a = keep.tile([P, 2048], F32)
+        z_b = keep.tile([P, 2048], F32)
         ob_a = keep.tile([P, 8, XW], F32)
         ob_b = keep.tile([P, 8, XW], F32)
+        oa_a = keep.tile([P, 8, XW], F32)
+        oa_b = keep.tile([P, 8, XW], F32)
         z_tiles = (z_a, z_b)
         ob_tiles = (ob_a, ob_b)
+        oa_tiles = (oa_a, oa_b)
 
         make_identity(nc, ident[:])
         ctx.enter_context(tc.manual_schedule())
@@ -124,11 +128,9 @@ def tile_fast2order_de_conv_t_kernel(tc, x, W, grad_out, out):
             load_chunk(1, 1)
             load_chunk(2, 1)
             load_x(nc.sync, both, 0, 16, XW)
-            nc.gpsimd.memset(fring[:, 0:GRID], 0.0)
-            for t in z_tiles:
-                nc.gpsimd.memset(t[:], 0.0)
-            for t in ob_tiles:
-                nc.gpsimd.memset(t[:], 0.0)
+            nc.vector.memset(fring[:, 0:GRID], 0.0)
+            for t in z_tiles + ob_tiles + oa_tiles:
+                nc.vector.memset(t[:], 0.0)
             pads = [(0, 1)] + [(FRAME * n + XW, 2) for n in range(NIMG)]
             for row0, cnt in pads:
                 cols = slice(row0 * GRID, (row0 + cnt) * GRID)
@@ -154,17 +156,27 @@ def tile_fast2order_de_conv_t_kernel(tc, x, W, grad_out, out):
             nc.vector.quantize_mx(out=w_codes[:, 0:256].bitcast(E4X4), scales=w_scales[:, 0:256], in_=w_grp[:, 0:1024])
             nc.vector.quantize_mx(out=w_codes[:, 256:768].bitcast(E4X4), scales=w_scales[:, 256:768], in_=w_grp[:, 1024:3072])
 
-        epool = ctx.enter_context(tc.tile_pool(name="epool", bufs=3))
+        epool = ctx.enter_context(tc.tile_pool(name="epool", bufs=2))
         opool = ctx.enter_context(tc.tile_pool(name="opool", bufs=2))
 
         def regroup(u):
             raw = raws[u // 2]
             off = 512 * (u % 2)
             grouped = grpp.tile([P, 2048], BF16, name="grouped", align_bytes=64)
+            s_cols = 512 if u < 2 else S_COLS
             nc.scalar.copy(
-                out=grouped[:].rearrange("p (c i t) -> p c t i", i=4, t=4),
-                in_=raw[:, :, off:off + 512].rearrange("p t (c i) -> p c t i", i=4),
+                out=grouped[:, 0:4 * s_cols].rearrange("p (c i t) -> p c t i", i=4, t=4),
+                in_=raw[:, :, off:off + s_cols].rearrange("p t (c i) -> p c t i", i=4),
             )
+            if s_cols < 512:
+                nc.gpsimd.tensor_scalar(
+                    out=grouped[:, 4 * s_cols:2048].rearrange("p (c i t) -> p c t i", i=4, t=4),
+                    in0=raw[:, :, off + s_cols:off + 512].rearrange("p t (c i) -> p c t i", i=4),
+                    scalar1=1.0,
+                    scalar2=0.0,
+                    op0=MULT,
+                    op1=ADD,
+                )
             groups[u] = grouped
             if u % 2 == 1 and u // 2 + 3 < 16:
                 load_chunk(u // 2 + 3, 1)
@@ -208,7 +220,8 @@ def tile_fast2order_de_conv_t_kernel(tc, x, W, grad_out, out):
             passes(beta, b, (2, 3, 4, 5))
             e0 = epool.tile([P, 512], F32, name="e0")
             nc.vector.tensor_tensor(out=rows_of(e0[:]), in0=rows_of(beta[:]), in1=xb_rows[:, r0:r0 + 8, 0:GRID], op=MULT)
-            nc.gpsimd.tensor_tensor(out=e0[:], in0=e0[:], in1=e1[:], op=ADD)
+            adder = nc.vector if b == NBLK - 1 else nc.gpsimd
+            adder.tensor_tensor(out=e0[:], in0=e0[:], in1=e1[:], op=ADD)
             es[b] = e0
 
         def first_t(b):
@@ -221,37 +234,32 @@ def tile_fast2order_de_conv_t_kernel(tc, x, W, grad_out, out):
                 nc.tensor.matmul(out=ps2[:, cols], lhsT=e0[:, cols], rhs=ident[:], is_transpose=True, start=False, stop=True)
             ps2s[b] = ps2
 
-        def z_view(b):
-            z = z_tiles[(b // 4) % 2]
-            return z[:].rearrange("p (q i k c) -> p q i k c", q=4, i=2, k=4)[:, :, :, b % 4, :]
-
-        def ps2_view(b, jz):
-            return ps2s[b][:].rearrange("p (q i j c) -> p q i j c", q=4, i=2, j=2)[:, :, :, jz, :]
-
         def evac2_copy(b):
-            nc.scalar.copy(out=z_view(b), in_=ps2_view(b, 0))
-
-        def z_add(b):
-            nc.vector.tensor_tensor(out=z_view(b), in0=ps2_view(b, 1), in1=z_view(b), op=ADD)
+            z = z_tiles[(b // 4) % 2]
+            nc.scalar.copy(
+                out=z[:].rearrange("p (g k c) -> p g k c", g=16, k=4)[:, :, b % 4, :],
+                in_=ps2s[b][:].rearrange("p (g c) -> p g c", g=16),
+            )
 
         def second_t(sb):
             z = z_tiles[sb % 2]
             ps3a = fps3.tile([P, 512], F32, name="ps3a")
             ps3b = fps3.tile([P, 512], F32, name="ps3b")
-            for pr in range(4):
-                nc.tensor.transpose(out=ps3b[:, pr * P:(pr + 1) * P], in_=z[:, pr * 256 + P:pr * 256 + 2 * P], identity=ident[:])
-            for pr in range(4):
-                nc.tensor.transpose(out=ps3a[:, pr * P:(pr + 1) * P], in_=z[:, pr * 256:pr * 256 + P], identity=ident[:])
+            for iz, ps3 in ((1, ps3b), (0, ps3a)):
+                for pr in range(4):
+                    for jz in range(2):
+                        c0 = ((pr * 2 + iz) * 2 + jz) * P
+                        nc.tensor.matmul(out=ps3[:, pr * P:(pr + 1) * P], lhsT=z[:, c0:c0 + P], rhs=ident[:], is_transpose=True, start=(jz == 0), stop=(jz == 1))
             ps3s[sb] = (ps3a, ps3b)
 
         def ps3_copy(sb):
             nc.scalar.copy(out=ob_tiles[sb % 2][:, :, 1:XW], in_=rows_of(ps3s[sb][1][:]))
+            nc.scalar.copy(out=oa_tiles[sb % 2][:, :, 0:GRID], in_=rows_of(ps3s[sb][0][:]))
 
         def final(sb):
-            ob = ob_tiles[sb % 2]
             o = opool.tile([P, 8, XW], F32, name="o")
-            nc.vector.tensor_tensor(out=o[:, :, 0:GRID], in0=rows_of(ps3s[sb][0][:]), in1=ob[:, :, 0:GRID], op=ADD)
-            nc.vector.tensor_copy(out=o[:, :, GRID:XW], in_=ob[:, :, GRID:XW])
+            adder = nc.vector if sb == (NBLK - 1) // 4 else nc.gpsimd
+            adder.tensor_tensor(out=o[:], in0=oa_tiles[sb % 2][:], in1=ob_tiles[sb % 2][:], op=ADD)
             for k in range(min(4, NBLK - 4 * sb)):
                 for k0, cnt, n, r0 in row_segments(4 * sb + k):
                     nc.sync.dma_start(
@@ -272,8 +280,6 @@ def tile_fast2order_de_conv_t_kernel(tc, x, W, grad_out, out):
                 load_x(nc.sync, both, (s + 6) // 8, 0, XW)
             if 0 <= s + 1 < 32:
                 quantise(s + 1)
-            if 0 <= s - 2 < NBLK:
-                z_add(s - 2)
             if (s - 3) in last_of:
                 final(last_of[s - 3])
             if 0 <= s < NBLK:

@@ -26,7 +26,6 @@ FRAME = 66
 NBLK = 33
 CODE_ROWS = 265
 XR_ROWS = 266
-S_COLS = 384
 
 PASSES = (
     (1, 0, False), (1, 0, True),
@@ -67,15 +66,12 @@ def tile_fast2order_de_conv_t_kernel(tc, x, W, grad_out, out):
         ident = keep.tile([P, P], F32)
         swap = keep.tile([P, P], F32)
         fring = keep.tile([P, 33 * GRID], F32)
-        z_a = keep.tile([P, 2048], F32)
-        z_b = keep.tile([P, 2048], F32)
+        z_a = keep.tile([P, 1024], F32)
+        z_b = keep.tile([P, 1024], F32)
         ob_a = keep.tile([P, 8, XW], F32)
         ob_b = keep.tile([P, 8, XW], F32)
-        oa_a = keep.tile([P, 8, XW], F32)
-        oa_b = keep.tile([P, 8, XW], F32)
         z_tiles = (z_a, z_b)
         ob_tiles = (ob_a, ob_b)
-        oa_tiles = (oa_a, oa_b)
 
         make_identity(nc, ident[:])
         ctx.enter_context(tc.manual_schedule())
@@ -128,9 +124,11 @@ def tile_fast2order_de_conv_t_kernel(tc, x, W, grad_out, out):
             load_chunk(1, 1)
             load_chunk(2, 1)
             load_x(nc.sync, both, 0, 16, XW)
-            nc.vector.memset(fring[:, 0:GRID], 0.0)
-            for t in z_tiles + ob_tiles + oa_tiles:
-                nc.vector.memset(t[:], 0.0)
+            nc.gpsimd.memset(fring[:, 0:GRID], 0.0)
+            for t in z_tiles:
+                nc.gpsimd.memset(t[:], 0.0)
+            for t in ob_tiles:
+                nc.gpsimd.memset(t[:], 0.0)
             pads = [(0, 1)] + [(FRAME * n + XW, 2) for n in range(NIMG)]
             for row0, cnt in pads:
                 cols = slice(row0 * GRID, (row0 + cnt) * GRID)
@@ -156,27 +154,17 @@ def tile_fast2order_de_conv_t_kernel(tc, x, W, grad_out, out):
             nc.vector.quantize_mx(out=w_codes[:, 0:256].bitcast(E4X4), scales=w_scales[:, 0:256], in_=w_grp[:, 0:1024])
             nc.vector.quantize_mx(out=w_codes[:, 256:768].bitcast(E4X4), scales=w_scales[:, 256:768], in_=w_grp[:, 1024:3072])
 
-        epool = ctx.enter_context(tc.tile_pool(name="epool", bufs=2))
+        epool = ctx.enter_context(tc.tile_pool(name="epool", bufs=3))
         opool = ctx.enter_context(tc.tile_pool(name="opool", bufs=2))
 
         def regroup(u):
             raw = raws[u // 2]
             off = 512 * (u % 2)
             grouped = grpp.tile([P, 2048], BF16, name="grouped", align_bytes=64)
-            s_cols = 512 if u < 2 else S_COLS
             nc.scalar.copy(
-                out=grouped[:, 0:4 * s_cols].rearrange("p (c i t) -> p c t i", i=4, t=4),
-                in_=raw[:, :, off:off + s_cols].rearrange("p t (c i) -> p c t i", i=4),
+                out=grouped[:].rearrange("p (c i t) -> p c t i", i=4, t=4),
+                in_=raw[:, :, off:off + 512].rearrange("p t (c i) -> p c t i", i=4),
             )
-            if s_cols < 512:
-                nc.gpsimd.tensor_scalar(
-                    out=grouped[:, 4 * s_cols:2048].rearrange("p (c i t) -> p c t i", i=4, t=4),
-                    in0=raw[:, :, off + s_cols:off + 512].rearrange("p t (c i) -> p c t i", i=4),
-                    scalar1=1.0,
-                    scalar2=0.0,
-                    op0=MULT,
-                    op1=ADD,
-                )
             groups[u] = grouped
             if u % 2 == 1 and u // 2 + 3 < 16:
                 load_chunk(u // 2 + 3, 1)
@@ -220,8 +208,7 @@ def tile_fast2order_de_conv_t_kernel(tc, x, W, grad_out, out):
             passes(beta, b, (2, 3, 4, 5))
             e0 = epool.tile([P, 512], F32, name="e0")
             nc.vector.tensor_tensor(out=rows_of(e0[:]), in0=rows_of(beta[:]), in1=xb_rows[:, r0:r0 + 8, 0:GRID], op=MULT)
-            adder = nc.vector if b == NBLK - 1 else nc.gpsimd
-            adder.tensor_tensor(out=e0[:], in0=e0[:], in1=e1[:], op=ADD)
+            nc.gpsimd.tensor_tensor(out=e0[:], in0=e0[:], in1=e1[:], op=ADD)
             es[b] = e0
 
         def first_t(b):
@@ -234,32 +221,37 @@ def tile_fast2order_de_conv_t_kernel(tc, x, W, grad_out, out):
                 nc.tensor.matmul(out=ps2[:, cols], lhsT=e0[:, cols], rhs=ident[:], is_transpose=True, start=False, stop=True)
             ps2s[b] = ps2
 
-        def evac2_copy(b):
+        def z_view(b):
             z = z_tiles[(b // 4) % 2]
-            nc.scalar.copy(
-                out=z[:].rearrange("p (g k c) -> p g k c", g=16, k=4)[:, :, b % 4, :],
-                in_=ps2s[b][:].rearrange("p (g c) -> p g c", g=16),
-            )
+            return z[:].rearrange("p (q i k c) -> p q i k c", q=4, i=2, k=4)[:, :, :, b % 4, :]
+
+        def ps2_view(b, jz):
+            return ps2s[b][:].rearrange("p (q i j c) -> p q i j c", q=4, i=2, j=2)[:, :, :, jz, :]
+
+        def evac2_copy(b):
+            nc.scalar.copy(out=z_view(b), in_=ps2_view(b, 0))
+
+        def z_add(b):
+            nc.vector.tensor_tensor(out=z_view(b), in0=ps2_view(b, 1), in1=z_view(b), op=ADD)
 
         def second_t(sb):
             z = z_tiles[sb % 2]
             ps3a = fps3.tile([P, 512], F32, name="ps3a")
             ps3b = fps3.tile([P, 512], F32, name="ps3b")
-            for iz, ps3 in ((1, ps3b), (0, ps3a)):
-                for pr in range(4):
-                    for jz in range(2):
-                        c0 = ((pr * 2 + iz) * 2 + jz) * P
-                        nc.tensor.matmul(out=ps3[:, pr * P:(pr + 1) * P], lhsT=z[:, c0:c0 + P], rhs=ident[:], is_transpose=True, start=(jz == 0), stop=(jz == 1))
+            for pr in range(4):
+                nc.tensor.transpose(out=ps3b[:, pr * P:(pr + 1) * P], in_=z[:, pr * 256 + P:pr * 256 + 2 * P], identity=ident[:])
+            for pr in range(4):
+                nc.tensor.transpose(out=ps3a[:, pr * P:(pr + 1) * P], in_=z[:, pr * 256:pr * 256 + P], identity=ident[:])
             ps3s[sb] = (ps3a, ps3b)
 
         def ps3_copy(sb):
             nc.scalar.copy(out=ob_tiles[sb % 2][:, :, 1:XW], in_=rows_of(ps3s[sb][1][:]))
-            nc.scalar.copy(out=oa_tiles[sb % 2][:, :, 0:GRID], in_=rows_of(ps3s[sb][0][:]))
 
         def final(sb):
+            ob = ob_tiles[sb % 2]
             o = opool.tile([P, 8, XW], F32, name="o")
-            adder = nc.vector if sb == (NBLK - 1) // 4 else nc.gpsimd
-            adder.tensor_tensor(out=o[:], in0=oa_tiles[sb % 2][:], in1=ob_tiles[sb % 2][:], op=ADD)
+            nc.vector.tensor_tensor(out=o[:, :, 0:GRID], in0=rows_of(ps3s[sb][0][:]), in1=ob[:, :, 0:GRID], op=ADD)
+            nc.vector.tensor_copy(out=o[:, :, GRID:XW], in_=ob[:, :, GRID:XW])
             for k in range(min(4, NBLK - 4 * sb)):
                 for k0, cnt, n, r0 in row_segments(4 * sb + k):
                     nc.sync.dma_start(
@@ -269,22 +261,24 @@ def tile_fast2order_de_conv_t_kernel(tc, x, W, grad_out, out):
 
         last_of = {min(4 * sb + 3, NBLK - 1): sb for sb in range((NBLK + 3) // 4)}
 
-        for s in range(-2, NBLK + 4):
-            if 0 <= s - 2 < NBLK:
-                evac2_copy(s - 2)
-            if (s - 3) in last_of:
-                ps3_copy(last_of[s - 3])
+        for s in range(-2, NBLK + 5):
+            if 0 <= s - 3 < NBLK:
+                evac2_copy(s - 3)
+            if (s - 4) in last_of:
+                ps3_copy(last_of[s - 4])
             if 0 <= s + 2 < 32:
                 regroup(s + 2)
             if s in (2, 10, 18):
                 load_x(nc.sync, both, (s + 6) // 8, 0, XW)
             if 0 <= s + 1 < 32:
                 quantise(s + 1)
-            if (s - 3) in last_of:
-                final(last_of[s - 3])
+            if 0 <= s - 3 < NBLK:
+                z_add(s - 3)
+            if (s - 4) in last_of:
+                final(last_of[s - 4])
             if 0 <= s < NBLK:
                 block(s)
-            if 0 <= s - 1 < NBLK:
-                first_t(s - 1)
-            if (s - 2) in last_of:
-                second_t(last_of[s - 2])
+            if 0 <= s - 2 < NBLK:
+                first_t(s - 2)
+            if (s - 3) in last_of:
+                second_t(last_of[s - 3])

@@ -26,6 +26,7 @@ FRAME = 66
 NBLK = 33
 CODE_ROWS = 265
 XR_ROWS = 266
+X0 = 1
 
 PASSES = (
     (1, 0, False), (1, 0, True),
@@ -59,8 +60,8 @@ def tile_fast2order_de_conv_t_kernel(tc, x, W, grad_out, out):
 
         g_codes = keep.tile([P, CODE_ROWS * GRID], U32, align_bytes=64)
         g_scales = keep.tile([P, CODE_ROWS * GRID], U8, align_bytes=64)
-        xr_b = keep.tile([P, XR_ROWS * XW], BF16)
-        xr_a = keep.tile([P, XR_ROWS * XW], BF16)
+        xr_b = keep.tile([P, XR_ROWS * XW + 2], BF16)
+        xr_a = keep.tile([P, XR_ROWS * XW + 2], BF16)
         w_codes = keep.tile([P, 768], U32, align_bytes=64)
         w_scales = keep.tile([P, 768], U8, align_bytes=64)
         ident = keep.tile([P, P], F32)
@@ -77,8 +78,8 @@ def tile_fast2order_de_conv_t_kernel(tc, x, W, grad_out, out):
         ctx.enter_context(tc.manual_schedule())
 
         img = FRAME * XW
-        xb_rows = xr_b[:].rearrange("p (r s) -> p r s", s=XW)
-        xa_rows = xr_a[:].rearrange("p (r s) -> p r s", s=XW)
+        xb_rows = xr_b[:, X0:X0 + XR_ROWS * XW].rearrange("p (r s) -> p r s", s=XW)
+        xa_rows = xr_a[:, X0:X0 + XR_ROWS * XW].rearrange("p (r s) -> p r s", s=XW)
         raws = {}
         groups = {}
         es = {}
@@ -98,12 +99,12 @@ def tile_fast2order_de_conv_t_kernel(tc, x, W, grad_out, out):
             raws[c] = raw
 
         def load_x(eng, which, n, row0, row1):
-            src = x[n].rearrange("c r s -> c (r s)")[:, row0 * XW:row1 * XW]
+            src = x[n].rearrange("c r s -> c (r s)")
             for q in range(4):
                 for xt, shift in ((xr_b, q % 2), (xr_a, q // 2)):
                     if xt in which:
-                        off = XW + img * n + row0 * XW - shift
-                        eng.dma_start(out=xt[CH * q:CH * (q + 1), off:off + (row1 - row0) * XW], in_=src)
+                        off = X0 + XW + img * n + row0 * XW
+                        eng.dma_start(out=xt[CH * q:CH * (q + 1), off:off + (row1 - row0) * XW - shift], in_=src[:, row0 * XW + shift:row1 * XW])
 
         wstage = tc.tile_pool(name="wstage", bufs=1)
         with wstage as wpool:
@@ -112,14 +113,14 @@ def tile_fast2order_de_conv_t_kernel(tc, x, W, grad_out, out):
             nc.scalar.dma_start(out=w_raw[:], in_=W.rearrange("(p t) f -> p t f", t=4))
             both = (xr_b, xr_a)
             for xt in both:
-                nc.gpsimd.memset(xt[:, 0:96], 0.0)
+                nc.gpsimd.memset(xt[:, 0:X0 + 96], 0.0)
             load_chunk(0, 2)
             load_x(nc.gpsimd, (xr_a,), 0, 0, 17)
             load_x(nc.sync, (xr_b,), 0, 0, 17)
             for xt in both:
                 for n in range(NIMG):
-                    lo = XW + img * n + XW * XW - 32
-                    hi = XW + img * (n + 1) + 32 if n < NIMG - 1 else XR_ROWS * XW
+                    lo = X0 + XW + img * n + XW * XW - 32
+                    hi = X0 + XW + img * (n + 1) + 32 if n < NIMG - 1 else XR_ROWS * XW + 2
                     nc.gpsimd.memset(xt[:, lo:hi], 0.0)
             load_chunk(1, 1)
             load_chunk(2, 1)
@@ -203,7 +204,7 @@ def tile_fast2order_de_conv_t_kernel(tc, x, W, grad_out, out):
             f0 = (1 + 8 * (b % 4)) * GRID
             nc.vector.tensor_tensor(out=rows_of(fring[:, f0:f0 + 512]), in0=rows_of(alpha[:]), in1=xa_rows[:, r0:r0 + 8, 0:GRID], op=MULT)
             if b % 4 == 3:
-                nc.vector.tensor_tensor(out=fring[:, 0:GRID], in0=alpha[:, 448:512], in1=xr_a[:, (r0 + 7) * XW:(r0 + 7) * XW + GRID], op=MULT)
+                nc.vector.tensor_tensor(out=fring[:, 0:GRID], in0=alpha[:, 448:512], in1=xr_a[:, X0 + (r0 + 7) * XW:X0 + (r0 + 7) * XW + GRID], op=MULT)
             beta = tps.tile([P, 512], F32, name="acc")
             passes(beta, b, (2, 3, 4, 5))
             e0 = epool.tile([P, 512], F32, name="e0")

@@ -26,6 +26,7 @@ FRAME = 66
 NBLK = 33
 CODE_ROWS = 265
 XR_ROWS = 266
+CHUNK = 2048
 X0 = 1
 
 PASSES = (
@@ -52,7 +53,7 @@ def tile_fast2order_de_conv_t_kernel(tc, x, W, grad_out, out):
     nc = tc.nc
     with ExitStack() as ctx:
         keep = ctx.enter_context(tc.tile_pool(name="keep", bufs=1))
-        rawp = ctx.enter_context(tc.tile_pool(name="rawp", bufs=3))
+        rawp = ctx.enter_context(tc.tile_pool(name="rawp", bufs=2))
         grpp = ctx.enter_context(tc.tile_pool(name="grpp", bufs=3))
         tps = ctx.enter_context(tc.psum_pool(name="tps", bufs=4))
         fps2 = ctx.enter_context(tc.psum_pool(name="fps2", bufs=2))
@@ -86,17 +87,14 @@ def tile_fast2order_de_conv_t_kernel(tc, x, W, grad_out, out):
         ps2s = {}
         ps3s = {}
 
-        def load_chunk(c, pieces):
-            n, h = divmod(c, 4)
-            raw = rawp.tile([P, 4, 1024], BF16, name="raw")
+        def load_chunk(c, bounds):
+            n, h = divmod(c, 2)
+            if c not in raws:
+                raw = rawp.tile([P, 4, CHUNK], BF16, name="raw")
+                raws[c] = raw
             src = grad_out[n].rearrange("(p t) y z -> p t (y z)", t=4)
-            w = 1024 // pieces
-            for k in range(pieces):
-                nc.sync.dma_start(
-                    out=raw[:, :, k * w:(k + 1) * w],
-                    in_=src[:, :, 1024 * h + k * w:1024 * h + (k + 1) * w],
-                )
-            raws[c] = raw
+            for lo, hi in bounds:
+                nc.sync.dma_start(out=raws[c][:, :, lo:hi], in_=src[:, :, CHUNK * h + lo:CHUNK * h + hi])
 
         def load_x(eng, which, n, row0, row1):
             src = x[n].rearrange("c r s -> c (r s)")
@@ -114,7 +112,7 @@ def tile_fast2order_de_conv_t_kernel(tc, x, W, grad_out, out):
             both = (xr_b, xr_a)
             for xt in both:
                 nc.gpsimd.memset(xt[:, 0:X0 + 96], 0.0)
-            load_chunk(0, 2)
+            load_chunk(0, ((0, 512), (512, 1024)))
             load_x(nc.gpsimd, (xr_a,), 0, 0, 17)
             load_x(nc.sync, (xr_b,), 0, 0, 17)
             for xt in both:
@@ -122,8 +120,8 @@ def tile_fast2order_de_conv_t_kernel(tc, x, W, grad_out, out):
                     lo = X0 + XW + img * n + XW * XW - 32
                     hi = X0 + XW + img * (n + 1) + 32 if n < NIMG - 1 else XR_ROWS * XW + 2
                     nc.gpsimd.memset(xt[:, lo:hi], 0.0)
-            load_chunk(1, 1)
-            load_chunk(2, 1)
+            load_chunk(0, ((1024, 2048),))
+            load_chunk(1, ((0, CHUNK),))
             load_x(nc.sync, both, 0, 16, XW)
             nc.gpsimd.memset(fring[:, 0:GRID], 0.0)
             for t in z_tiles:
@@ -159,16 +157,16 @@ def tile_fast2order_de_conv_t_kernel(tc, x, W, grad_out, out):
         opool = ctx.enter_context(tc.tile_pool(name="opool", bufs=2))
 
         def regroup(u):
-            raw = raws[u // 2]
-            off = 512 * (u % 2)
+            raw = raws[u // 4]
+            off = 512 * (u % 4)
             grouped = grpp.tile([P, 2048], BF16, name="grouped", align_bytes=64)
             nc.scalar.copy(
                 out=grouped[:].rearrange("p (c i t) -> p c t i", i=4, t=4),
                 in_=raw[:, :, off:off + 512].rearrange("p t (c i) -> p c t i", i=4),
             )
             groups[u] = grouped
-            if u % 2 == 1 and u // 2 + 3 < 16:
-                load_chunk(u // 2 + 3, 1)
+            if u % 4 == 3 and u // 4 + 2 < 8:
+                load_chunk(u // 4 + 2, ((0, CHUNK),))
 
         def quantise(u):
             n, j = divmod(u, 8)

@@ -53,20 +53,21 @@ def tile_fast2order_de_conv_t_kernel(tc, x, W, grad_out, out):
     nc = tc.nc
     with ExitStack() as ctx:
         keep = ctx.enter_context(tc.tile_pool(name="keep", bufs=1))
-        rawp = ctx.enter_context(tc.tile_pool(name="rawp", bufs=2))
+        rawp = ctx.enter_context(tc.tile_pool(name="rawp", bufs=3))
         grpp = ctx.enter_context(tc.tile_pool(name="grpp", bufs=3))
         tps = ctx.enter_context(tc.psum_pool(name="tps", bufs=4))
-        fps2 = ctx.enter_context(tc.psum_pool(name="fps2", bufs=2))
+        fps2 = ctx.enter_context(tc.psum_pool(name="fps2", bufs=1))
         fps3 = ctx.enter_context(tc.psum_pool(name="fps3", bufs=1))
+        xps = ctx.enter_context(tc.psum_pool(name="xps", bufs=1))
 
         g_codes = keep.tile([P, CODE_ROWS * GRID], U32, align_bytes=64)
         g_scales = keep.tile([P, CODE_ROWS * GRID], U8, align_bytes=64)
         xr_b = keep.tile([P, XR_ROWS * XW + 2], BF16)
-        xr_a = keep.tile([P, XR_ROWS * XW + 2], BF16)
         w_codes = keep.tile([P, 768], U32, align_bytes=64)
         w_scales = keep.tile([P, 768], U8, align_bytes=64)
         ident = keep.tile([P, P], F32)
         swap = keep.tile([P, P], F32)
+        swap_b = keep.tile([P, P], BF16)
         fring = keep.tile([P, 33 * GRID], F32)
         z_a = keep.tile([P, 1024], F32)
         z_b = keep.tile([P, 1024], F32)
@@ -80,10 +81,11 @@ def tile_fast2order_de_conv_t_kernel(tc, x, W, grad_out, out):
 
         img = FRAME * XW
         xb_rows = xr_b[:, X0:X0 + XR_ROWS * XW].rearrange("p (r s) -> p r s", s=XW)
-        xa_rows = xr_a[:, X0:X0 + XR_ROWS * XW].rearrange("p (r s) -> p r s", s=XW)
         raws = {}
         groups = {}
         es = {}
+        xa_banks = {}
+        xas = {}
         ps2s = {}
         ps3s = {}
 
@@ -94,35 +96,37 @@ def tile_fast2order_de_conv_t_kernel(tc, x, W, grad_out, out):
                 raws[c] = raw
             src = grad_out[n].rearrange("(p t) y z -> p t (y z)", t=4)
             for lo, hi in bounds:
-                nc.sync.dma_start(out=raws[c][:, :, lo:hi], in_=src[:, :, CHUNK * h + lo:CHUNK * h + hi])
+                if c == 0:
+                    dst = raws[c][:].rearrange("p t w -> p (t w)")[:, 4 * lo:4 * hi].rearrange("p (t w) -> p t w", t=4)
+                else:
+                    dst = raws[c][:, :, lo:hi]
+                nc.sync.dma_start(out=dst, in_=src[:, :, CHUNK * h + lo:CHUNK * h + hi])
 
-        def load_x(eng, which, n, row0, row1):
+        def load_x(n, row0, row1):
             src = x[n].rearrange("c r s -> c (r s)")
             for q in range(4):
-                for xt, shift in ((xr_b, q % 2), (xr_a, q // 2)):
-                    if xt in which:
-                        off = X0 + XW + img * n + row0 * XW
-                        eng.dma_start(out=xt[CH * q:CH * (q + 1), off:off + (row1 - row0) * XW - shift], in_=src[:, row0 * XW + shift:row1 * XW])
+                shift = q % 2
+                off = X0 + XW + img * n + row0 * XW
+                nc.sync.dma_start(out=xr_b[CH * q:CH * (q + 1), off:off + (row1 - row0) * XW - shift], in_=src[:, row0 * XW + shift:row1 * XW])
 
         wstage = tc.tile_pool(name="wstage", bufs=1)
         with wstage as wpool:
             w_raw = wpool.tile([P, 4, 512], BF16)
             w_grp = wpool.tile([P, 3072], BF16, align_bytes=64)
             nc.scalar.dma_start(out=w_raw[:], in_=W.rearrange("(p t) f -> p t f", t=4))
-            both = (xr_b, xr_a)
-            for xt in both:
-                nc.gpsimd.memset(xt[:, 0:X0 + 96], 0.0)
-            load_chunk(0, ((0, 512), (512, 1024)))
-            load_x(nc.gpsimd, (xr_a,), 0, 0, 17)
-            load_x(nc.sync, (xr_b,), 0, 0, 17)
-            for xt in both:
-                for n in range(NIMG):
-                    lo = X0 + XW + img * n + XW * XW - 32
-                    hi = X0 + XW + img * (n + 1) + 32 if n < NIMG - 1 else XR_ROWS * XW + 2
-                    nc.gpsimd.memset(xt[:, lo:hi], 0.0)
-            load_chunk(0, ((1024, 2048),))
+            nc.gpsimd.memset(xr_b[:, 0:X0 + 96], 0.0)
+            for n in range(NIMG):
+                lo = X0 + XW + img * n + XW * XW - 32
+                hi = X0 + XW + img * (n + 1) + 32 if n < NIMG - 1 else XR_ROWS * XW + 2
+                nc.gpsimd.memset(xr_b[:, lo:hi], 0.0)
+            load_chunk(0, ((0, 512),))
+            load_x(0, 0, 17)
+            load_chunk(0, ((512, 1024), (1024, 1536), (1536, 2048)))
+            load_x(0, 16, 33)
             load_chunk(1, ((0, CHUNK),))
-            load_x(nc.sync, both, 0, 16, XW)
+            load_x(0, 32, XW)
+            load_chunk(2, ((0, CHUNK),))
+            load_x(1, 0, XW)
             nc.gpsimd.memset(fring[:, 0:GRID], 0.0)
             for t in z_tiles:
                 nc.gpsimd.memset(t[:], 0.0)
@@ -137,6 +141,7 @@ def tile_fast2order_de_conv_t_kernel(tc, x, W, grad_out, out):
             nc.vector.tensor_copy(out=swap[:, 32:64], in_=ident[:, 64:96])
             nc.vector.tensor_copy(out=swap[:, 64:96], in_=ident[:, 32:64])
             nc.vector.tensor_copy(out=swap[:, 96:128], in_=ident[:, 96:128])
+            nc.vector.tensor_copy(out=swap_b[:], in_=swap[:])
 
             w_view = w_raw[:].rearrange("p t (c a b) -> p t c a b", a=4, b=4)
             for k, (dy, iy, transposed) in enumerate(PASSES):
@@ -155,18 +160,23 @@ def tile_fast2order_de_conv_t_kernel(tc, x, W, grad_out, out):
 
         epool = ctx.enter_context(tc.tile_pool(name="epool", bufs=3))
         opool = ctx.enter_context(tc.tile_pool(name="opool", bufs=2))
+        xap = ctx.enter_context(tc.tile_pool(name="xap", bufs=2))
 
         def regroup(u):
             raw = raws[u // 4]
             off = 512 * (u % 4)
+            if u < 4:
+                unit = raw[:].rearrange("p t w -> p (t w)")[:, 4 * off:4 * off + 2048].rearrange("p (t w) -> p t w", t=4)
+            else:
+                unit = raw[:, :, off:off + 512]
             grouped = grpp.tile([P, 2048], BF16, name="grouped", align_bytes=64)
             nc.scalar.copy(
                 out=grouped[:].rearrange("p (c i t) -> p c t i", i=4, t=4),
-                in_=raw[:, :, off:off + 512].rearrange("p t (c i) -> p c t i", i=4),
+                in_=unit.rearrange("p t (c i) -> p c t i", i=4),
             )
             groups[u] = grouped
-            if u % 4 == 3 and u // 4 + 2 < 8:
-                load_chunk(u // 4 + 2, ((0, CHUNK),))
+            if u % 4 == 3 and u // 4 + 3 < 8:
+                load_chunk(u // 4 + 3, ((0, CHUNK),))
 
         def quantise(u):
             n, j = divmod(u, 8)
@@ -200,15 +210,30 @@ def tile_fast2order_de_conv_t_kernel(tc, x, W, grad_out, out):
             e1 = epool.tile([P, 512], F32, name="e1")
             nc.vector.tensor_tensor(out=rows_of(e1[:]), in0=rows_of(alpha[:]), in1=xb_rows[:, r0 + 1:r0 + 9, 0:GRID], op=MULT)
             f0 = (1 + 8 * (b % 4)) * GRID
-            nc.vector.tensor_tensor(out=rows_of(fring[:, f0:f0 + 512]), in0=rows_of(alpha[:]), in1=xa_rows[:, r0:r0 + 8, 0:GRID], op=MULT)
+            xa0 = 512 * (b % 2)
+            xa = xas[b // 2]
+            nc.vector.tensor_tensor(out=fring[:, f0:f0 + 512], in0=alpha[:], in1=xa[:, xa0:xa0 + 512], op=MULT)
             if b % 4 == 3:
-                nc.vector.tensor_tensor(out=fring[:, 0:GRID], in0=alpha[:, 448:512], in1=xr_a[:, X0 + (r0 + 7) * XW:X0 + (r0 + 7) * XW + GRID], op=MULT)
+                nc.vector.tensor_tensor(out=fring[:, 0:GRID], in0=alpha[:, 448:512], in1=xa[:, xa0 + 448:xa0 + 512], op=MULT)
             beta = tps.tile([P, 512], F32, name="acc")
             passes(beta, b, (2, 3, 4, 5))
             e0 = epool.tile([P, 512], F32, name="e0")
             nc.vector.tensor_tensor(out=rows_of(e0[:]), in0=rows_of(beta[:]), in1=xb_rows[:, r0:r0 + 8, 0:GRID], op=MULT)
             nc.gpsimd.tensor_tensor(out=e0[:], in0=e0[:], in1=e1[:], op=ADD)
             es[b] = e0
+
+        def make_xa(pair):
+            bank = xps.tile([P, 1024], BF16, name="xa_bank")
+            for h in range(min(2, NBLK - 2 * pair)):
+                r0 = 1 + 8 * (2 * pair + h)
+                nc.tensor.matmul(out=rows_of(bank[:, 512 * h:512 * (h + 1)]), lhsT=swap_b[:], rhs=xb_rows[:, r0:r0 + 8, 0:GRID], start=True, stop=True)
+            xa_banks[pair] = bank
+
+        def copy_xa(pair):
+            w = 512 * min(2, NBLK - 2 * pair)
+            xa = xap.tile([P, 1024], BF16, name="xa")
+            nc.scalar.copy(out=xa[:, 0:w], in_=xa_banks[pair][:, 0:w])
+            xas[pair] = xa
 
         def first_t(b):
             e0 = es[b]
@@ -265,10 +290,12 @@ def tile_fast2order_de_conv_t_kernel(tc, x, W, grad_out, out):
                 evac2_copy(s - 3)
             if (s - 4) in last_of:
                 ps3_copy(last_of[s - 4])
+            if s % 2 == 1 and s + 1 < NBLK:
+                copy_xa((s + 1) // 2)
             if 0 <= s + 2 < 32:
                 regroup(s + 2)
-            if s in (2, 10, 18):
-                load_x(nc.sync, both, (s + 6) // 8, 0, XW)
+            if s in (5, 13):
+                load_x((s + 11) // 8, 0, XW)
             if 0 <= s + 1 < 32:
                 quantise(s + 1)
             if 0 <= s - 3 < NBLK:
@@ -277,6 +304,8 @@ def tile_fast2order_de_conv_t_kernel(tc, x, W, grad_out, out):
                 final(last_of[s - 4])
             if 0 <= s < NBLK:
                 block(s)
+            if s % 2 == 0 and s + 2 < NBLK:
+                make_xa((s + 2) // 2)
             if 0 <= s - 2 < NBLK:
                 first_t(s - 2)
             if (s - 3) in last_of:

@@ -26,6 +26,8 @@ FRAME = 66
 NBLK = 33
 CODE_ROWS = 265
 XR_ROWS = 266
+G_POS = 128
+G_FROM = 4
 CHUNK = 2048
 X0 = 1
 
@@ -162,19 +164,30 @@ def tile_fast2order_de_conv_t_kernel(tc, x, W, grad_out, out):
         opool = ctx.enter_context(tc.tile_pool(name="opool", bufs=2))
         xap = ctx.enter_context(tc.tile_pool(name="xap", bufs=2))
 
+        def regroup_g(u):
+            grouped = grpp.tile([P, 2048], BF16, name="grouped", align_bytes=64)
+            groups[u] = grouped
+            if u >= G_FROM:
+                off = 512 * (u % 4) + 512 - G_POS
+                nc.gpsimd.tensor_scalar(
+                    out=grouped[:, 2048 - 4 * G_POS:2048].rearrange("p (c t) -> p c t", t=4),
+                    in0=raws[u // 4][:, :, off:off + G_POS].rearrange("p t c -> p c t"),
+                    scalar1=1.0, scalar2=0.0, op0=MULT, op1=ADD,
+                )
+
         def regroup(u):
             raw = raws[u // 4]
             off = 512 * (u % 4)
+            npos = 512 if u < G_FROM else 512 - G_POS
             if u < 4:
                 unit = raw[:].rearrange("p t w -> p (t w)")[:, 4 * off:4 * off + 2048].rearrange("p (t w) -> p t w", t=4)
             else:
-                unit = raw[:, :, off:off + 512]
-            grouped = grpp.tile([P, 2048], BF16, name="grouped", align_bytes=64)
+                unit = raw[:, :, off:off + npos]
+            grouped = groups[u]
             nc.scalar.copy(
-                out=grouped[:].rearrange("p (c i t) -> p c t i", i=4, t=4),
+                out=grouped[:, 0:4 * npos].rearrange("p (c i t) -> p c t i", i=4, t=4),
                 in_=unit.rearrange("p t (c i) -> p c t i", i=4),
             )
-            groups[u] = grouped
             if u % 4 == 3 and u // 4 + 3 < 8:
                 load_chunk(u // 4 + 3, ((0, CHUNK),))
 
@@ -285,13 +298,15 @@ def tile_fast2order_de_conv_t_kernel(tc, x, W, grad_out, out):
 
         last_of = {min(4 * sb + 3, NBLK - 1): sb for sb in range((NBLK + 3) // 4)}
 
-        for s in range(-2, NBLK + 5):
+        for s in range(-3, NBLK + 5):
             if 0 <= s - 3 < NBLK:
                 evac2_copy(s - 3)
             if (s - 4) in last_of:
                 ps3_copy(last_of[s - 4])
-            if s % 2 == 1 and s + 1 < NBLK:
+            if s % 2 == 1 and 0 <= s + 1 < NBLK:
                 copy_xa((s + 1) // 2)
+            if 0 <= s + 3 < 32:
+                regroup_g(s + 3)
             if 0 <= s + 2 < 32:
                 regroup(s + 2)
             if s in (5, 13):
@@ -304,7 +319,7 @@ def tile_fast2order_de_conv_t_kernel(tc, x, W, grad_out, out):
                 final(last_of[s - 4])
             if 0 <= s < NBLK:
                 block(s)
-            if s % 2 == 0 and s + 2 < NBLK:
+            if s % 2 == 0 and 0 <= s + 2 < NBLK:
                 make_xa((s + 2) // 2)
             if 0 <= s - 2 < NBLK:
                 first_t(s - 2)

@@ -57,8 +57,8 @@ def tile_fast2order_de_conv_t_kernel(tc, x, W, grad_out, out):
         keep = ctx.enter_context(tc.tile_pool(name="keep", bufs=1))
         rawp = ctx.enter_context(tc.tile_pool(name="rawp", bufs=3))
         grpp = ctx.enter_context(tc.tile_pool(name="grpp", bufs=3))
-        tps = ctx.enter_context(tc.psum_pool(name="tps", bufs=4))
-        fps2 = ctx.enter_context(tc.psum_pool(name="fps2", bufs=1))
+        tps = ctx.enter_context(tc.psum_pool(name="tps", bufs=3))
+        fps2 = ctx.enter_context(tc.psum_pool(name="fps2", bufs=2))
         fps3 = ctx.enter_context(tc.psum_pool(name="fps3", bufs=1))
         xps = ctx.enter_context(tc.psum_pool(name="xps", bufs=1))
 
@@ -70,6 +70,7 @@ def tile_fast2order_de_conv_t_kernel(tc, x, W, grad_out, out):
         ident = keep.tile([P, P], F32)
         swap = keep.tile([P, P], F32)
         swap_b = keep.tile([P, P], BF16)
+        warm = keep.tile([P, 1], F32)
         fring = keep.tile([P, 33 * GRID], F32)
         z_a = keep.tile([P, 1024], F32)
         z_b = keep.tile([P, 1024], F32)
@@ -86,6 +87,7 @@ def tile_fast2order_de_conv_t_kernel(tc, x, W, grad_out, out):
         raws = {}
         groups = {}
         es = {}
+        e1s = {}
         xa_banks = {}
         xas = {}
         ps2s = {}
@@ -116,6 +118,7 @@ def tile_fast2order_de_conv_t_kernel(tc, x, W, grad_out, out):
             w_raw = wpool.tile([P, 4, 512], BF16)
             w_grp = wpool.tile([P, 3072], BF16, align_bytes=64)
             nc.scalar.dma_start(out=w_raw[:], in_=W.rearrange("(p t) f -> p t f", t=4))
+            nc.scalar.copy(out=warm[:], in_=ident[:, 0:1])
             nc.gpsimd.memset(xr_b[:, 0:X0 + 96], 0.0)
             for n in range(NIMG):
                 lo = X0 + XW + img * n + XW * XW - 32
@@ -164,29 +167,29 @@ def tile_fast2order_de_conv_t_kernel(tc, x, W, grad_out, out):
         opool = ctx.enter_context(tc.tile_pool(name="opool", bufs=2))
         xap = ctx.enter_context(tc.tile_pool(name="xap", bufs=2))
 
+        def unit_of(u):
+            raw = raws[u // 4]
+            off = 512 * (u % 4)
+            if u < 4:
+                return raw[:].rearrange("p t w -> p (t w)")[:, 4 * off:4 * off + 2048].rearrange("p (t w) -> p t w", t=4)
+            return raw[:, :, off:off + 512]
+
         def regroup_g(u):
             grouped = grpp.tile([P, 2048], BF16, name="grouped", align_bytes=64)
             groups[u] = grouped
             if u >= G_FROM:
-                off = 512 * (u % 4) + 512 - G_POS
                 nc.gpsimd.tensor_scalar(
                     out=grouped[:, 2048 - 4 * G_POS:2048].rearrange("p (c t) -> p c t", t=4),
-                    in0=raws[u // 4][:, :, off:off + G_POS].rearrange("p t c -> p c t"),
+                    in0=unit_of(u)[:, :, 512 - G_POS:512].rearrange("p t c -> p c t"),
                     scalar1=1.0, scalar2=0.0, op0=MULT, op1=ADD,
                 )
 
         def regroup(u):
-            raw = raws[u // 4]
-            off = 512 * (u % 4)
             npos = 512 if u < G_FROM else 512 - G_POS
-            if u < 4:
-                unit = raw[:].rearrange("p t w -> p (t w)")[:, 4 * off:4 * off + 2048].rearrange("p (t w) -> p t w", t=4)
-            else:
-                unit = raw[:, :, off:off + npos]
             grouped = groups[u]
             nc.scalar.copy(
                 out=grouped[:, 0:4 * npos].rearrange("p (c i t) -> p c t i", i=4, t=4),
-                in_=unit.rearrange("p t (c i) -> p c t i", i=4),
+                in_=unit_of(u)[:, :, 0:npos].rearrange("p t (c i) -> p c t i", i=4),
             )
             if u % 4 == 3 and u // 4 + 3 < 8:
                 load_chunk(u // 4 + 3, ((0, CHUNK),))
@@ -232,8 +235,10 @@ def tile_fast2order_de_conv_t_kernel(tc, x, W, grad_out, out):
             passes(beta, b, (2, 3, 4, 5))
             e0 = epool.tile([P, 512], F32, name="e0")
             nc.vector.tensor_tensor(out=rows_of(e0[:]), in0=rows_of(beta[:]), in1=xb_rows[:, r0:r0 + 8, 0:GRID], op=MULT)
-            nc.gpsimd.tensor_tensor(out=e0[:], in0=e0[:], in1=e1[:], op=ADD)
+            if b < NBLK - 1:
+                nc.gpsimd.tensor_tensor(out=e0[:], in0=e0[:], in1=e1[:], op=ADD)
             es[b] = e0
+            e1s[b] = e1
 
         def make_xa(pair):
             bank = xps.tile([P, 1024], BF16, name="xa_bank")
@@ -255,7 +260,9 @@ def tile_fast2order_de_conv_t_kernel(tc, x, W, grad_out, out):
                 cols = slice(pr * P, (pr + 1) * P)
                 f0 = (8 * (b % 4) + 2 * pr) * GRID
                 nc.tensor.matmul(out=ps2[:, cols], lhsT=fring[:, f0:f0 + P], rhs=swap[:], is_transpose=True, start=True, stop=False)
-                nc.tensor.matmul(out=ps2[:, cols], lhsT=e0[:, cols], rhs=ident[:], is_transpose=True, start=False, stop=True)
+                nc.tensor.matmul(out=ps2[:, cols], lhsT=e0[:, cols], rhs=ident[:], is_transpose=True, start=False, stop=b < NBLK - 1)
+                if b == NBLK - 1:
+                    nc.tensor.matmul(out=ps2[:, cols], lhsT=e1s[b][:, cols], rhs=ident[:], is_transpose=True, start=False, stop=True)
             ps2s[b] = ps2
 
         def z_view(b):
@@ -266,10 +273,15 @@ def tile_fast2order_de_conv_t_kernel(tc, x, W, grad_out, out):
             return ps2s[b][:].rearrange("p (q i j c) -> p q i j c", q=4, i=2, j=2)[:, :, :, jz, :]
 
         def evac2_copy(b):
-            nc.scalar.copy(out=z_view(b), in_=ps2_view(b, 0))
+            if b < NBLK - 1:
+                nc.scalar.copy(out=z_view(b), in_=ps2_view(b, 0))
 
         def z_add(b):
-            nc.vector.tensor_tensor(out=z_view(b), in0=ps2_view(b, 1), in1=z_view(b), op=ADD)
+            if b < NBLK - 1:
+                nc.vector.tensor_tensor(out=z_view(b), in0=ps2_view(b, 1), in1=z_view(b), op=ADD)
+            else:
+                pairs = ps2s[b][:].rearrange("p (q i j c) -> p q i c j", q=4, i=2, j=2)
+                nc.vector.tensor_reduce(out=z_view(b), in_=pairs, axis=mybir.AxisListType.X, op=ADD)
 
         def second_t(sb):
             z = z_tiles[sb % 2]
@@ -282,7 +294,10 @@ def tile_fast2order_de_conv_t_kernel(tc, x, W, grad_out, out):
             ps3s[sb] = (ps3a, ps3b)
 
         def ps3_copy(sb):
-            nc.scalar.copy(out=ob_tiles[sb % 2][:, :, 1:XW], in_=rows_of(ps3s[sb][1][:]))
+            if 4 * sb + 4 < NBLK:
+                nc.scalar.copy(out=ob_tiles[sb % 2][:, :, 1:XW], in_=rows_of(ps3s[sb][1][:]))
+            else:
+                nc.vector.tensor_copy(out=ob_tiles[sb % 2][:, :, 1:XW], in_=rows_of(ps3s[sb][1][:]))
 
         def final(sb):
             ob = ob_tiles[sb % 2]

@@ -188,8 +188,8 @@ def tile_fast2order_de_conv_t_kernel(tc, x, W, grad_out, out):
             npos = 512 if u < G_FROM else 512 - G_POS
             grouped = groups[u]
             nc.scalar.copy(
-                out=grouped[:, 0:4 * npos].rearrange("p (c i t) -> p c t i", i=4, t=4),
-                in_=unit_of(u)[:, :, 0:npos].rearrange("p t (c i) -> p c t i", i=4),
+                out=grouped[:, 0:4 * npos].rearrange("p (c i t) -> p c t i", i=8, t=4),
+                in_=unit_of(u)[:, :, 0:npos].rearrange("p t (c i) -> p c t i", i=8),
             )
             if u % 4 == 3 and u // 4 + 3 < 8:
                 load_chunk(u // 4 + 3, ((0, CHUNK),))

from contextlib import ExitStack

import concourse.bass as bass
import concourse.mybir as mybir
import concourse.tile as tile
from concourse.masks import make_identity

F32 = mybir.dt.float32
BF16 = mybir.dt.bfloat16
U32 = mybir.dt.uint32
U8 = mybir.dt.uint8
I32 = mybir.dt.int32
E4X4 = mybir.dt.float8_e4m3fn_x4
E5X4 = mybir.dt.float8_e5m2_x4
ADD = mybir.AluOpType.add
MULT = mybir.AluOpType.mult

FLOPS = 2 * 4 * 4096 * 512 * 512

P = 128
NIMG = 4
CH = 32
GRID = 64
XW = 65
FRAME = 66
NBLK = 33
CODE_ROWS = 265
XR_ROWS = 266
G_POS = 128
G_FROM = 4
CHUNK = 2048
X0 = 1

PASSES = (
    (1, 0, False), (1, 0, True),
    (0, 0, False), (0, 0, True), (0, 1, False), (0, 1, True),
)


def row_segments(b):
    segs = []
    for k in range(8):
        n, r = divmod(8 * b + k, FRAME)
        if r == XW:
            continue
        if segs and segs[-1][2] == n and segs[-1][0] + segs[-1][1] == k:
            last = segs[-1]
            segs[-1] = (last[0], last[1] + 1, last[2], last[3])
        else:
            segs.append((k, 1, n, r))
    return segs


def tile_fast2order_de_conv_t_kernel(tc, x, W, grad_out, out):
    nc = tc.nc
    with ExitStack() as ctx:
        keep = ctx.enter_context(tc.tile_pool(name="keep", bufs=1))
        rawp = ctx.enter_context(tc.tile_pool(name="rawp", bufs=3))
        grpp = ctx.enter_context(tc.tile_pool(name="grpp", bufs=3))
        tps = ctx.enter_context(tc.psum_pool(name="tps", bufs=3))
        fps2 = ctx.enter_context(tc.psum_pool(name="fps2", bufs=2))
        fps3 = ctx.enter_context(tc.psum_pool(name="fps3", bufs=1))
        xps = ctx.enter_context(tc.psum_pool(name="xps", bufs=1))

        g_codes = keep.tile([P, CODE_ROWS * GRID], U32, align_bytes=64)
        g_scales = keep.tile([P, CODE_ROWS * GRID], U8, align_bytes=64)
        xr_b = keep.tile([P, XR_ROWS * XW + 2], BF16)
        w_codes = keep.tile([P, 768], U32, align_bytes=64)
        w_scales = keep.tile([P, 768], U8, align_bytes=64)
        ident = keep.tile([P, P], F32)
        swap = keep.tile([P, P], F32)
        swap_b = keep.tile([P, P], BF16)
        warm = keep.tile([P, 1], F32)
        fring = keep.tile([P, 33 * GRID], F32)
        z_a = keep.tile([P, 1024], F32)
        z_b = keep.tile([P, 1024], F32)
        ob_a = keep.tile([P, 8, XW], F32)
        ob_b = keep.tile([P, 8, XW], F32)
        z_tiles = (z_a, z_b)
        ob_tiles = (ob_a, ob_b)

        make_identity(nc, ident[:])
        ctx.enter_context(tc.manual_schedule())

        img = FRAME * XW
        xb_rows = xr_b[:, X0:X0 + XR_ROWS * XW].rearrange("p (r s) -> p r s", s=XW)
        raws = {}
        groups = {}
        es = {}
        e1s = {}
        xa_banks = {}
        xas = {}
        ps2s = {}
        ps3s = {}

        def load_chunk(c, bounds):
            n, h = divmod(c, 2)
            if c not in raws:
                raw = rawp.tile([P, 4, CHUNK], BF16, name="raw")
                raws[c] = raw
            src = grad_out[n].rearrange("(p t) y z -> p t (y z)", t=4)
            for lo, hi in bounds:
                if c == 0:
                    dst = raws[c][:].rearrange("p t w -> p (t w)")[:, 4 * lo:4 * hi].rearrange("p (t w) -> p t w", t=4)
                else:
                    dst = raws[c][:, :, lo:hi]
                nc.sync.dma_start(out=dst, in_=src[:, :, CHUNK * h + lo:CHUNK * h + hi])

        def load_x(n, row0, row1):
            src = x[n].rearrange("c r s -> c (r s)")
            for q in range(4):
                shift = q % 2
                off = X0 + XW + img * n + row0 * XW
                nc.sync.dma_start(out=xr_b[CH * q:CH * (q + 1), off:off + (row1 - row0) * XW - shift], in_=src[:, row0 * XW + shift:row1 * XW])

        wstage = tc.tile_pool(name="wstage", bufs=1)
        with wstage as wpool:
            w_raw = wpool.tile([P, 4, 512], BF16)
            w_grp = wpool.tile([P, 3072], BF16, align_bytes=64)
            nc.scalar.dma_start(out=w_raw[:], in_=W.rearrange("(p t) f -> p t f", t=4))
            nc.scalar.copy(out=warm[:], in_=ident[:, 0:1])
            nc.gpsimd.memset(xr_b[:, 0:X0 + 96], 0.0)
            for n in range(NIMG):
                lo = X0 + XW + img * n + XW * XW - 32
                hi = X0 + XW + img * (n + 1) + 32 if n < NIMG - 1 else XR_ROWS * XW + 2
                nc.gpsimd.memset(xr_b[:, lo:hi], 0.0)
            load_chunk(0, ((0, 512),))
            load_x(0, 0, 17)
            load_chunk(0, ((512, 1024), (1024, 1536), (1536, 2048)))
            load_x(0, 16, 33)
            load_chunk(1, ((0, CHUNK),))
            load_x(0, 32, XW)
            load_chunk(2, ((0, CHUNK),))
            load_x(1, 0, XW)
            nc.gpsimd.memset(fring[:, 0:GRID], 0.0)
            for t in z_tiles:
                nc.gpsimd.memset(t[:], 0.0)
            for t in ob_tiles:
                nc.gpsimd.memset(t[:], 0.0)
            pads = [(0, 1)] + [(FRAME * n + XW, 2) for n in range(NIMG)]
            for row0, cnt in pads:
                cols = slice(row0 * GRID, (row0 + cnt) * GRID)
                nc.vector.memset(g_codes[:, cols].bitcast(I32), 0)
                nc.vector.memset(g_scales[:, cols].bitcast(I32), 0)
            nc.vector.tensor_copy(out=swap[:, 0:32], in_=ident[:, 0:32])
            nc.vector.tensor_copy(out=swap[:, 32:64], in_=ident[:, 64:96])
            nc.vector.tensor_copy(out=swap[:, 64:96], in_=ident[:, 32:64])
            nc.vector.tensor_copy(out=swap[:, 96:128], in_=ident[:, 96:128])
            nc.vector.tensor_copy(out=swap_b[:], in_=swap[:])

            w_view = w_raw[:].rearrange("p t (c a b) -> p t c a b", a=4, b=4)
            for k, (dy, iy, transposed) in enumerate(PASSES):
                i0 = 2 * iy
                j0 = 2 * (iy + dy)
                if transposed:
                    src = w_view[:, :, :, j0:j0 + 2, i0:i0 + 2].rearrange("p t c j i -> p i j c t")
                else:
                    src = w_view[:, :, :, i0:i0 + 2, j0:j0 + 2].rearrange("p t c i j -> p i j c t")
                nc.vector.tensor_copy(
                    out=w_grp[:, k * 512:(k + 1) * 512].rearrange("p (i j c t) -> p i j c t", i=2, j=2, t=4),
                    in_=src,
                )
            nc.vector.quantize_mx(out=w_codes[:, 0:256].bitcast(E4X4), scales=w_scales[:, 0:256], in_=w_grp[:, 0:1024])
            nc.vector.quantize_mx(out=w_codes[:, 256:768].bitcast(E4X4), scales=w_scales[:, 256:768], in_=w_grp[:, 1024:3072])

        epool = ctx.enter_context(tc.tile_pool(name="epool", bufs=3))
        opool = ctx.enter_context(tc.tile_pool(name="opool", bufs=2))
        xap = ctx.enter_context(tc.tile_pool(name="xap", bufs=2))

        def unit_of(u):
            raw = raws[u // 4]
            off = 512 * (u % 4)
            if u < 4:
                return raw[:].rearrange("p t w -> p (t w)")[:, 4 * off:4 * off + 2048].rearrange("p (t w) -> p t w", t=4)
            return raw[:, :, off:off + 512]

        def regroup_g(u):
            grouped = grpp.tile([P, 2048], BF16, name="grouped", align_bytes=64)
            groups[u] = grouped
            if u >= G_FROM:
                nc.gpsimd.tensor_scalar(
                    out=grouped[:, 2048 - 4 * G_POS:2048].rearrange("p (c t) -> p c t", t=4),
                    in0=unit_of(u)[:, :, 512 - G_POS:512].rearrange("p t c -> p c t"),
                    scalar1=1.0, scalar2=0.0, op0=MULT, op1=ADD,
                )

        def regroup(u):
            npos = 512 if u < G_FROM else 512 - G_POS
            grouped = groups[u]
            nc.scalar.copy(
                out=grouped[:, 0:4 * npos].rearrange("p (c i t) -> p c t i", i=8, t=4),
                in_=unit_of(u)[:, :, 0:npos].rearrange("p t (c i) -> p c t i", i=8),
            )
            if u % 4 == 3 and u // 4 + 3 < 8:
                load_chunk(u // 4 + 3, ((0, CHUNK),))

        def quantise(u):
            n, j = divmod(u, 8)
            col0 = (FRAME * n + 1 + 8 * j) * GRID
            nc.vector.quantize_mx(
                out=g_codes[:, col0:col0 + 512].bitcast(E5X4),
                scales=g_scales[:, col0:col0 + 512],
                in_=groups[u][:],
            )

        def passes(acc, b, ks):
            for pos, k in enumerate(ks):
                w0 = (8 * b + 1 - PASSES[k][1]) * GRID
                nc.tensor.matmul_mx(
                    out=acc[:],
                    lhsT=w_codes[:, k * P:(k + 1) * P].bitcast(E4X4),
                    lhsT_scale=w_scales[:, k * P:(k + 1) * P],
                    rhs=g_codes[:, w0:w0 + 512].bitcast(E5X4),
                    rhs_scale=g_scales[:, w0:w0 + 512],
                    start=(pos == 0),
                    stop=(pos == len(ks) - 1),
                )

        def rows_of(ap):
            return ap.rearrange("p (r u) -> p r u", u=GRID)

        def block(b):
            r0 = 1 + 8 * b
            alpha = tps.tile([P, 512], F32, name="acc")
            passes(alpha, b, (0, 1))
            e1 = epool.tile([P, 512], F32, name="e1")
            nc.vector.tensor_tensor(out=rows_of(e1[:]), in0=rows_of(alpha[:]), in1=xb_rows[:, r0 + 1:r0 + 9, 0:GRID], op=MULT)
            f0 = (1 + 8 * (b % 4)) * GRID
            xa0 = 512 * (b % 2)
            xa = xas[b // 2]
            nc.vector.tensor_tensor(out=fring[:, f0:f0 + 512], in0=alpha[:], in1=xa[:, xa0:xa0 + 512], op=MULT)
            if b % 4 == 3:
                nc.vector.tensor_tensor(out=fring[:, 0:GRID], in0=alpha[:, 448:512], in1=xa[:, xa0 + 448:xa0 + 512], op=MULT)
            beta = tps.tile([P, 512], F32, name="acc")
            passes(beta, b, (2, 3, 4, 5))
            e0 = epool.tile([P, 512], F32, name="e0")
            nc.vector.tensor_tensor(out=rows_of(e0[:]), in0=rows_of(beta[:]), in1=xb_rows[:, r0:r0 + 8, 0:GRID], op=MULT)
            if b < NBLK - 1:
                nc.gpsimd.tensor_tensor(out=e0[:], in0=e0[:], in1=e1[:], op=ADD)
            es[b] = e0
            e1s[b] = e1

        def make_xa(pair):
            bank = xps.tile([P, 1024], BF16, name="xa_bank")
            for h in range(min(2, NBLK - 2 * pair)):
                r0 = 1 + 8 * (2 * pair + h)
                nc.tensor.matmul(out=rows_of(bank[:, 512 * h:512 * (h + 1)]), lhsT=swap_b[:], rhs=xb_rows[:, r0:r0 + 8, 0:GRID], start=True, stop=True)
            xa_banks[pair] = bank

        def copy_xa(pair):
            w = 512 * min(2, NBLK - 2 * pair)
            xa = xap.tile([P, 1024], BF16, name="xa")
            nc.scalar.copy(out=xa[:, 0:w], in_=xa_banks[pair][:, 0:w])
            xas[pair] = xa

        def first_t(b):
            e0 = es[b]
            ps2 = fps2.tile([P, 512], F32, name="ps2")
            for pr in range(4):
                cols = slice(pr * P, (pr + 1) * P)
                f0 = (8 * (b % 4) + 2 * pr) * GRID
                nc.tensor.matmul(out=ps2[:, cols], lhsT=fring[:, f0:f0 + P], rhs=swap[:], is_transpose=True, start=True, stop=False)
                nc.tensor.matmul(out=ps2[:, cols], lhsT=e0[:, cols], rhs=ident[:], is_transpose=True, start=False, stop=b < NBLK - 1)
                if b == NBLK - 1:
                    nc.tensor.matmul(out=ps2[:, cols], lhsT=e1s[b][:, cols], rhs=ident[:], is_transpose=True, start=False, stop=True)
            ps2s[b] = ps2

        def z_view(b):
            z = z_tiles[(b // 4) % 2]
            return z[:].rearrange("p (q i k c) -> p q i k c", q=4, i=2, k=4)[:, :, :, b % 4, :]

        def ps2_view(b, jz):
            return ps2s[b][:].rearrange("p (q i j c) -> p q i j c", q=4, i=2, j=2)[:, :, :, jz, :]

        def evac2_copy(b):
            if b < NBLK - 1:
                nc.scalar.copy(out=z_view(b), in_=ps2_view(b, 0))

        def z_add(b):
            if b < NBLK - 1:
                nc.vector.tensor_tensor(out=z_view(b), in0=ps2_view(b, 1), in1=z_view(b), op=ADD)
            else:
                pairs = ps2s[b][:].rearrange("p (q i j c) -> p q i c j", q=4, i=2, j=2)
                nc.vector.tensor_reduce(out=z_view(b), in_=pairs, axis=mybir.AxisListType.X, op=ADD)

        def second_t(sb):
            z = z_tiles[sb % 2]
            ps3a = fps3.tile([P, 512], F32, name="ps3a")
            ps3b = fps3.tile([P, 512], F32, name="ps3b")
            for pr in range(4):
                nc.tensor.transpose(out=ps3b[:, pr * P:(pr + 1) * P], in_=z[:, pr * 256 + P:pr * 256 + 2 * P], identity=ident[:])
            for pr in range(4):
                nc.tensor.transpose(out=ps3a[:, pr * P:(pr + 1) * P], in_=z[:, pr * 256:pr * 256 + P], identity=ident[:])
            ps3s[sb] = (ps3a, ps3b)

        def ps3_copy(sb):
            if 4 * sb + 4 < NBLK:
                nc.scalar.copy(out=ob_tiles[sb % 2][:, :, 1:XW], in_=rows_of(ps3s[sb][1][:]))
            else:
                nc.vector.tensor_copy(out=ob_tiles[sb % 2][:, :, 1:XW], in_=rows_of(ps3s[sb][1][:]))

        def final(sb):
            ob = ob_tiles[sb % 2]
            o = opool.tile([P, 8, XW], F32, name="o")
            nc.vector.tensor_tensor(out=o[:, :, 0:GRID], in0=rows_of(ps3s[sb][0][:]), in1=ob[:, :, 0:GRID], op=ADD)
            nc.vector.tensor_copy(out=o[:, :, GRID:XW], in_=ob[:, :, GRID:XW])
            for k in range(min(4, NBLK - 4 * sb)):
                for k0, cnt, n, r0 in row_segments(4 * sb + k):
                    nc.sync.dma_start(
                        out=out[n, :, r0:r0 + cnt, :],
                        in_=o[CH * k:CH * (k + 1), k0:k0 + cnt, :],
                    )

        last_of = {min(4 * sb + 3, NBLK - 1): sb for sb in range((NBLK + 3) // 4)}

        for s in range(-3, NBLK + 5):
            if 0 <= s - 3 < NBLK:
                evac2_copy(s - 3)
            if (s - 4) in last_of:
                ps3_copy(last_of[s - 4])
            if s % 2 == 1 and 0 <= s + 1 < NBLK:
                copy_xa((s + 1) // 2)
            if 0 <= s + 3 < 32:
                regroup_g(s + 3)
            if 0 <= s + 2 < 32:
                regroup(s + 2)
            if s in (5, 13):
                load_x((s + 11) // 8, 0, XW)
            if 0 <= s + 1 < 32:
                quantise(s + 1)
            if 0 <= s - 3 < NBLK:
                z_add(s - 3)
            if (s - 4) in last_of:
                final(last_of[s - 4])
            if 0 <= s < NBLK:
                block(s)
            if s % 2 == 0 and 0 <= s + 2 < NBLK:
                make_xa((s + 2) // 2)
            if 0 <= s - 2 < NBLK:
                first_t(s - 2)
            if (s - 3) in last_of:
                second_t(last_of[s - 3])
